import numpy as np
import ml_dtypes


def mxq(x, axis, fmt="e4m3"):
    dtype, down = {"e4m3": (ml_dtypes.float8_e4m3fn, 7), "e5m2": (ml_dtypes.float8_e5m2, 14)}[fmt]
    v = np.moveaxis(np.asarray(x, np.float32).astype(ml_dtypes.bfloat16).astype(np.float64), axis, -1)
    blocks = v.reshape(v.shape[:-1] + (-1, 32))
    amax = np.abs(blocks).max(-1, keepdims=True)
    byte = np.maximum(np.where(amax > 0, np.frexp(amax)[1] - 1 + 127, 0) - down, 1)
    scale = np.exp2(byte - 127.0)
    codes = (blocks / scale).astype(np.float32).astype(dtype).astype(np.float64)
    return np.moveaxis((codes * scale).reshape(v.shape), -1, axis)


WIDE = False


def mx_kscale(k):
    if not WIDE:
        return np.ones(k)
    levels = np.array([10, -10, 5, -5, 0])
    a = np.random.permutation(np.resize(levels, k // 512 * 4)).reshape(k // 512, 4)
    idx = np.arange(k)
    return np.exp2(a[idx // 512, idx % 128 // 32])


BF16 = ml_dtypes.bfloat16


def bf(x):
    return np.asarray(x, np.float32).astype(BF16)


def f64(x):
    return np.asarray(x).astype(np.float64)


B, C, T, E, H = 1, 512, 4, 1024, 8
D = E // H
S = C * T


def setup_inputs():
    t = mx_kscale(E)
    th = t.reshape(H, D)
    mag = 2.0 + 2.0 * np.random.random((B, H, C, T, D))
    sgn = np.where(np.random.random((B, H, C, T, D)) < 0.5, -1.0, 1.0)
    return {"q": bf(np.random.standard_normal((B, H, C, T, D)) * 2.0),
            "k_means": bf(np.random.standard_normal((B, H, C, D))),
            "v_means": bf(np.random.uniform(-1.0, 1.0, (B, H, C, D)) * th[None, :, None, :]),
            "intra": bf(sgn * mag * th[None, :, None, None, :]),
            "wo": bf(np.random.standard_normal((E, E)) / np.sqrt(E) / t[None, :]),
            "bo": bf(np.random.standard_normal(E) * 0.3)}


def reference(q, k_means, v_means, intra, wo, bo):
    s = f64(q).reshape(B, H, S, D) @ f64(k_means).transpose(0, 1, 3, 2) * (1.0 / np.sqrt(D))
    causal = np.repeat(np.arange(C), T)[:, None] >= np.arange(C)[None, :]
    s = np.where(causal[None, None], s, -np.inf)
    e = np.exp(s - s.max(-1, keepdims=True))
    inter = (mxq(e, 3, "e4m3") @ mxq(f64(v_means), 2, "e4m3")) / e.sum(-1, keepdims=True)
    fused = (f64(intra).reshape(B, H, S, D) + inter).transpose(0, 2, 1, 3).reshape(B, S, E)
    return (mxq(fused, 2, "e4m3") @ mxq(f64(wo), 1, "e4m3").T) + f64(bo)

@@ -1,0 +1,265 @@
+import math
+from contextlib import ExitStack
+
+import concourse.mybir as mybir
+from concourse.masks import make_identity
+
+BF16 = mybir.dt.bfloat16
+F32 = mybir.dt.float32
+U32 = mybir.dt.uint32
+U8 = mybir.dt.uint8
+FP8X4 = mybir.dt.float8_e4m3fn_x4
+ACT = mybir.ActivationFunctionType
+ALU = mybir.AluOpType
+AXIS = mybir.AxisListType
+
+P = 128
+PACK = 4
+HEADS = 8
+D = 128
+CHUNKS = 512
+PLACES = 4
+TOKENS = CHUNKS * PLACES
+E = HEADS * D
+TILES = TOKENS // P
+TILE_CHUNKS = P // PLACES
+GROUPS = E // (P * PACK)
+HALF = 512
+SCALE = 1.0 / math.sqrt(D)
+PAIRS = HEADS // 2
+SETS = 2
+MASKED = -1.0e30
+
+FLOPS = 2 * HEADS * TOKENS * CHUNKS * D * 2 + 2 * TOKENS * E * E
+
+
+def tile_chunkedattention_pa_kernel(tc, q, k_means, v_means, intra, wo, bo, out):
+    nc = tc.nc
+    q_rows = q.rearrange("b h c t d -> (b h) (c t) d")
+    intra_rows = intra.rearrange("b h c t d -> (b h) (c t) d")
+    k_blocks = k_means.rearrange("b h (t p) d -> t p (b h) d", p=P)
+    v_blocks = v_means.rearrange("b h (t p) d -> t p (b h) d", p=P)
+    out_rows = out.rearrange("b s o -> (b s) o")
+
+    with ExitStack() as ctx:
+        keep = ctx.enter_context(tc.tile_pool(name="keep", bufs=1))
+        work = ctx.enter_context(tc.tile_pool(name="work", bufs=3))
+        small = ctx.enter_context(tc.tile_pool(name="small", bufs=4))
+        store = ctx.enter_context(tc.tile_pool(name="store", bufs=3))
+        turn_ps = ctx.enter_context(tc.psum_pool(name="turn_ps", bufs=2))
+        score_ps = ctx.enter_context(tc.psum_pool(name="score_ps", bufs=3))
+        inter_ps = ctx.enter_context(tc.psum_pool(name="inter_ps", bufs=1))
+        out_ps = ctx.enter_context(tc.psum_pool(name="out_ps", bufs=2))
+
+        k_sb = keep.tile([P, PACK, HEADS, D], BF16)
+        v_sb = keep.tile([P, PACK, HEADS, D], BF16)
+        wo_sb = keep.tile([P, E // P, E], BF16)
+        bias = keep.tile([P, E], BF16)
+        q_sb = [keep.tile([P, HEADS, D], BF16, name="q_sb%d" % i) for i in range(TILES)]
+        intra_sb = [keep.tile([P, HEADS, D], BF16, name="intra_sb%d" % i) for i in range(TILES)]
+
+        def load_tile(i):
+            rows = slice(i * P, (i + 1) * P)
+            nc.sync.dma_start(out=q_sb[i][:], in_=q_rows[:, rows, :].rearrange("h p d -> p h d"))
+            nc.sync.dma_start(out=intra_sb[i][:], in_=intra_rows[:, rows, :].rearrange("h p d -> p h d"))
+
+        nc.sync.dma_start(out=k_sb[:, 0], in_=k_blocks[0])
+        load_tile(0)
+        for t in range(PACK):
+            nc.sync.dma_start(out=v_sb[:, t], in_=v_blocks[t])
+        nc.sync.dma_start(out=wo_sb[:], in_=wo.rearrange("(a p) k -> p a k", p=P))
+        nc.sync.dma_start(out=bias[:], in_=bo.partition_broadcast(P))
+        for t in range(1, PACK):
+            nc.sync.dma_start(out=k_sb[:, t], in_=k_blocks[t])
+        for i in range(1, TILES):
+            load_tile(i)
+
+        ident = keep.tile([P, P], BF16)
+        make_identity(nc, ident[:])
+        mask_f32 = keep.tile([P, TILE_CHUNKS], F32)
+        nc.gpsimd.memset(mask_f32[:], 0.0)
+        nc.gpsimd.affine_select(
+            out=mask_f32[:],
+            in_=mask_f32[:],
+            pattern=[[-PLACES, TILE_CHUNKS]],
+            compare_op=ALU.is_ge,
+            fill=MASKED,
+            base=0,
+            channel_multiplier=1,
+        )
+        mask = keep.tile([P, TILE_CHUNKS], BF16)
+        nc.vector.tensor_copy(out=mask[:], in_=mask_f32[:])
+
+        e_sb = [keep.tile([P, CHUNKS], BF16, name="e_sb%d" % n) for n in range(SETS * HEADS)]
+        e_grouped = [keep.tile([P, 2, P, PACK], BF16, name="e_grouped%d" % n, align_bytes=64) for n in range(SETS * PAIRS)]
+        for n in range(SETS * HEADS):
+            nc.gpsimd.memset(e_sb[n][:], 0.0)
+        for n in range(SETS * PAIRS):
+            nc.vector.memset(e_grouped[n][:], 0.0)
+
+        k_t = keep.tile([P, HEADS, CHUNKS], BF16)
+
+        def turn_k(t):
+            k_ps = turn_ps.tile([P, HEADS, P], BF16, tag="turn")
+            for h in range(HEADS):
+                nc.tensor.transpose(k_ps[:, h, :], k_sb[:, t, h, :], ident[:])
+            nc.vector.tensor_copy(out=k_t[:, :, t * P : (t + 1) * P], in_=k_ps[:])
+
+        v_grouped = keep.tile([P, HEADS * D, PACK], BF16, align_bytes=64)
+        v_codes = keep.tile([P, HEADS * D], U32, align_bytes=64)
+        v_scales = keep.tile([P, HEADS * D], U8, align_bytes=64)
+
+        def quantise_v():
+            nc.vector.tensor_copy(out=v_grouped[:], in_=v_sb[:].rearrange("p t h d -> p (h d) t"))
+            nc.vector.quantize_mx(
+                out=v_codes[:].bitcast(FP8X4),
+                scales=v_scales[:],
+                in_=v_grouped[:].rearrange("p c t -> p (c t)"),
+            )
+
+        wo_grouped = keep.tile([P, GROUPS, E, PACK], BF16, align_bytes=64)
+        wo_codes = keep.tile([P, GROUPS, E], U32, align_bytes=64)
+        wo_scales = keep.tile([P, GROUPS, E], U8, align_bytes=64)
+
+        def quantise_wo():
+            for a in range(E // P):
+                wo_ps = turn_ps.tile([P, GROUPS * PACK, P], BF16, tag="turn")
+                for b in range(GROUPS * PACK):
+                    nc.tensor.transpose(wo_ps[:, b, :], wo_sb[:, a, b * P : (b + 1) * P], ident[:])
+                copy = nc.scalar.copy if a % 2 == 0 else nc.vector.tensor_copy
+                copy(
+                    out=wo_grouped[:, :, a * P : (a + 1) * P, :],
+                    in_=wo_ps[:].rearrange("p (g t) o -> p g o t", t=PACK),
+                )
+            for g in range(GROUPS):
+                nc.vector.quantize_mx(
+                    out=wo_codes[:, g, :].bitcast(FP8X4),
+                    scales=wo_scales[:, g, :],
+                    in_=wo_grouped[:, g].rearrange("p o t -> p (o t)"),
+                )
+
+        q_t = {}
+        sums = {}
+        over_sum = {}
+        fused = {}
+        i_ps = {}
+
+        def turn_q(i):
+            q_ps = turn_ps.tile([P, HEADS, P], BF16, tag="turn")
+            for h in range(HEADS):
+                nc.tensor.transpose(q_ps[:, h, :], q_sb[i][:, h, :], ident[:])
+            q_t[i] = work.tile([P, HEADS, P], BF16, name="q_t")
+            nc.scalar.copy(out=q_t[i][:], in_=q_ps[:])
+            sums[i] = small.tile([P, HEADS], F32, name="sums")
+
+        def softmax(i, a):
+            width = TILE_CHUNKS * (i + 1)
+            for h in (2 * a, 2 * a + 1):
+                s_ps = score_ps.tile([P, CHUNKS], F32)
+                nc.tensor.matmul(s_ps[:, 0:width], lhsT=q_t[i][:, h, :], rhs=k_t[:, h, 0:width], start=True, stop=False)
+                nc.tensor.matmul(s_ps[:, width - TILE_CHUNKS : width], lhsT=ident[:], rhs=mask[:], start=False, stop=True)
+                top = small.tile([P, 1], F32)
+                nc.vector.tensor_reduce(out=top[:], in_=s_ps[:, 0:width], axis=AXIS.X, op=ALU.max)
+                shift = small.tile([P, 1], F32)
+                nc.vector.tensor_scalar_mul(out=shift[:], in0=top[:], scalar1=-SCALE)
+                nc.scalar.activation(
+                    out=e_sb[(i % SETS) * HEADS + h][:, 0:width],
+                    in_=s_ps[:, 0:width],
+                    func=ACT.Exp,
+                    bias=shift[:],
+                    scale=SCALE,
+                    accum_out=sums[i][:, h : h + 1],
+                )
+
+        def attend(i, a):
+            blocks = i // PACK + 1
+            if a == 0:
+                over_sum[i] = small.tile([P, HEADS], F32, name="over_sum")
+                nc.vector.reciprocal(out=over_sum[i][:], in_=sums[i][:])
+                fused[i] = work.tile([P, HEADS, D], BF16, name="fused")
+            if a % 2 == 0:
+                i_ps[i] = inter_ps.tile([P, PACK, D], F32, name="i_ps")
+            grouped = e_grouped[(i % SETS) * PAIRS + a]
+            e_ps = turn_ps.tile([P, 2, PACK, P], BF16, tag="turn")
+            for b in range(2):
+                for t in range(blocks):
+                    nc.tensor.transpose(e_ps[:, b, t, :], e_sb[(i % SETS) * HEADS + 2 * a + b][:, t * P : (t + 1) * P], ident[:])
+            nc.scalar.copy(
+                out=grouped[:, :, :, 0:blocks],
+                in_=e_ps[:, :, 0:blocks, :].rearrange("p b t r -> p b r t"),
+            )
+            e_codes = work.tile([P, 2, P], U32, align_bytes=64)
+            e_scales = work.tile([P, 2, P], U8, align_bytes=64)
+            nc.vector.quantize_mx(
+                out=e_codes[:].rearrange("p b r -> p (b r)").bitcast(FP8X4),
+                scales=e_scales[:].rearrange("p b r -> p (b r)"),
+                in_=grouped[:].rearrange("p b r t -> p (b r t)"),
+            )
+            for b in range(2):
+                h = 2 * a + b
+                nc.tensor.matmul_mx(
+                    out=i_ps[i][:, h % PACK, :],
+                    lhsT=e_codes[:, b, :].bitcast(FP8X4),
+                    lhsT_scale=e_scales[:, b, :],
+                    rhs=v_codes[:, h * D : (h + 1) * D].bitcast(FP8X4),
+                    rhs_scale=v_scales[:, h * D : (h + 1) * D],
+                    start=True,
+                    stop=True,
+                )
+            for b in range(2):
+                h = 2 * a + b
+                nc.vector.scalar_tensor_tensor(
+                    out=fused[i][:, h, :],
+                    in0=i_ps[i][:, h % PACK, :],
+                    scalar=over_sum[i][:, h : h + 1],
+                    in1=intra_sb[i][:, h, :],
+                    op0=ALU.mult,
+                    op1=ALU.add,
+                )
+
+        def project(i):
+            f_ps = turn_ps.tile([P, HEADS, P], BF16, tag="turn")
+            for h in range(HEADS):
+                nc.tensor.transpose(f_ps[:, h, :], fused[i][:, h, :], ident[:])
+            f_grouped = work.tile([P, GROUPS, P, PACK], BF16, align_bytes=64)
+            nc.scalar.copy(out=f_grouped[:], in_=f_ps[:].rearrange("p (g t) r -> p g r t", t=PACK))
+            f_codes = work.tile([P, GROUPS, P], U32, align_bytes=64)
+            f_scales = work.tile([P, GROUPS, P], U8, align_bytes=64)
+            nc.vector.quantize_mx(
+                out=f_codes[:].rearrange("p g r -> p (g r)").bitcast(FP8X4),
+                scales=f_scales[:].rearrange("p g r -> p (g r)"),
+                in_=f_grouped[:].rearrange("p g r t -> p (g r t)"),
+            )
+            result = store.tile([P, E], F32)
+            for n in range(E // HALF):
+                cols = slice(n * HALF, (n + 1) * HALF)
+                o_ps = out_ps.tile([P, HALF], F32)
+                for g in range(GROUPS):
+                    nc.tensor.matmul_mx(
+                        out=o_ps[:],
+                        lhsT=f_codes[:, g, :].bitcast(FP8X4),
+                        lhsT_scale=f_scales[:, g, :],
+                        rhs=wo_codes[:, g, cols].bitcast(FP8X4),
+                        rhs_scale=wo_scales[:, g, cols],
+                        start=(g == 0),
+                        stop=(g == GROUPS - 1),
+                    )
+                nc.vector.tensor_tensor(out=result[:, cols], in0=o_ps[:], in1=bias[:, cols], op=ALU.add)
+            nc.sync.dma_start(out=out_rows[i * P : (i + 1) * P, :], in_=result[:])
+
+        turn_k(0)
+        turn_q(0)
+        quantise_v()
+        quantise_wo()
+        for n in range(TILES + 2):
+            if 0 <= n - 2:
+                project(n - 2)
+            if n + 1 < TILES:
+                if (n + 1) % PACK == 0:
+                    turn_k((n + 1) // PACK)
+                turn_q(n + 1)
+            for a in range(PAIRS):
+                if 0 <= n - 1 < TILES:
+                    attend(n - 1, a)
+                if n < TILES:
+                    softmax(n, a)

@@ -27,7 +27,6 @@ GROUPS = E // (P * PACK)
 HALF = 512
 SCALE = 1.0 / math.sqrt(D)
 PAIRS = HEADS // 2
-SETS = 2
 MASKED = -1.0e30
 
 FLOPS = 2 * HEADS * TOKENS * CHUNKS * D * 2 + 2 * TOKENS * E * E
@@ -42,14 +41,15 @@ def tile_chunkedattention_pa_kernel(tc, q, k_means, v_means, intra, wo, bo, out)
     out_rows = out.rearrange("b s o -> (b s) o")
 
     with ExitStack() as ctx:
+        ctx.enter_context(tc.manual_schedule())
         keep = ctx.enter_context(tc.tile_pool(name="keep", bufs=1))
-        work = ctx.enter_context(tc.tile_pool(name="work", bufs=3))
-        small = ctx.enter_context(tc.tile_pool(name="small", bufs=4))
+        work = ctx.enter_context(tc.tile_pool(name="work", bufs=4))
+        small = ctx.enter_context(tc.tile_pool(name="small", bufs=6))
         store = ctx.enter_context(tc.tile_pool(name="store", bufs=3))
-        turn_ps = ctx.enter_context(tc.psum_pool(name="turn_ps", bufs=2))
+        turn_ps = ctx.enter_context(tc.psum_pool(name="turn_ps", bufs=3))
         score_ps = ctx.enter_context(tc.psum_pool(name="score_ps", bufs=3))
         inter_ps = ctx.enter_context(tc.psum_pool(name="inter_ps", bufs=1))
-        out_ps = ctx.enter_context(tc.psum_pool(name="out_ps", bufs=2))
+        out_ps = ctx.enter_context(tc.psum_pool(name="out_ps", bufs=1))
 
         k_sb = keep.tile([P, PACK, HEADS, D], BF16)
         v_sb = keep.tile([P, PACK, HEADS, D], BF16)
@@ -58,21 +58,26 @@ def tile_chunkedattention_pa_kernel(tc, q, k_means, v_means, intra, wo, bo, out)
         q_sb = [keep.tile([P, HEADS, D], BF16, name="q_sb%d" % i) for i in range(TILES)]
         intra_sb = [keep.tile([P, HEADS, D], BF16, name="intra_sb%d" % i) for i in range(TILES)]
 
-        def load_tile(i):
-            rows = slice(i * P, (i + 1) * P)
-            nc.sync.dma_start(out=q_sb[i][:], in_=q_rows[:, rows, :].rearrange("h p d -> p h d"))
-            nc.sync.dma_start(out=intra_sb[i][:], in_=intra_rows[:, rows, :].rearrange("h p d -> p h d"))
+        def load_rows(tiles, rows, i):
+            nc.sync.dma_start(out=tiles[i][:], in_=rows[:, i * P : (i + 1) * P, :].rearrange("h p d -> p h d"))
 
+        wo_blocks = wo.rearrange("(a p) k -> a p k", p=P)
         nc.sync.dma_start(out=k_sb[:, 0], in_=k_blocks[0])
-        load_tile(0)
+        load_rows(q_sb, q_rows, 0)
+        load_rows(q_sb, q_rows, 1)
         for t in range(PACK):
             nc.sync.dma_start(out=v_sb[:, t], in_=v_blocks[t])
-        nc.sync.dma_start(out=wo_sb[:], in_=wo.rearrange("(a p) k -> p a k", p=P))
-        nc.sync.dma_start(out=bias[:], in_=bo.partition_broadcast(P))
-        for t in range(1, PACK):
-            nc.sync.dma_start(out=k_sb[:, t], in_=k_blocks[t])
-        for i in range(1, TILES):
-            load_tile(i)
+        for i in range(TILES):
+            if i < PACK:
+                for a in (2 * i, 2 * i + 1):
+                    nc.sync.dma_start(out=wo_sb[:, a, :], in_=wo_blocks[a])
+            if i + 2 < TILES:
+                load_rows(q_sb, q_rows, i + 2)
+            load_rows(intra_sb, intra_rows, i)
+            if i % PACK == 0 and i // PACK + 1 < PACK:
+                nc.sync.dma_start(out=k_sb[:, i // PACK + 1], in_=k_blocks[i // PACK + 1])
+            if i == PACK:
+                nc.sync.dma_start(out=bias[:], in_=bo.partition_broadcast(P))
 
         ident = keep.tile([P, P], BF16)
         make_identity(nc, ident[:])
@@ -90,20 +95,24 @@ def tile_chunkedattention_pa_kernel(tc, q, k_means, v_means, intra, wo, bo, out)
         mask = keep.tile([P, TILE_CHUNKS], BF16)
         nc.vector.tensor_copy(out=mask[:], in_=mask_f32[:])
 
-        e_sb = [keep.tile([P, CHUNKS], BF16, name="e_sb%d" % n) for n in range(SETS * HEADS)]
-        e_grouped = [keep.tile([P, 2, P, PACK], BF16, name="e_grouped%d" % n, align_bytes=64) for n in range(SETS * PAIRS)]
-        for n in range(SETS * HEADS):
+        e_sb = [keep.tile([P, CHUNKS], BF16, name="e_sb%d" % n) for n in range(HEADS)]
+        e_grouped = [keep.tile([P, 2, P, PACK], BF16, name="e_grouped%d" % n, align_bytes=64) for n in range(PAIRS)]
+        for n in range(HEADS):
             nc.gpsimd.memset(e_sb[n][:], 0.0)
-        for n in range(SETS * PAIRS):
+        for n in range(PAIRS):
             nc.vector.memset(e_grouped[n][:], 0.0)
 
         k_t = keep.tile([P, HEADS, CHUNKS], BF16)
 
+        k_ps = {}
+
         def turn_k(t):
-            k_ps = turn_ps.tile([P, HEADS, P], BF16, tag="turn")
+            k_ps[t] = turn_ps.tile([P, HEADS, P], BF16, tag="turn", name="k_ps")
             for h in range(HEADS):
-                nc.tensor.transpose(k_ps[:, h, :], k_sb[:, t, h, :], ident[:])
-            nc.vector.tensor_copy(out=k_t[:, :, t * P : (t + 1) * P], in_=k_ps[:])
+                nc.tensor.transpose(k_ps[t][:, h, :], k_sb[:, t, h, :], ident[:])
+
+        def keep_k(t):
+            nc.vector.tensor_copy(out=k_t[:, :, t * P : (t + 1) * P], in_=k_ps[t][:])
 
         v_grouped = keep.tile([P, HEADS * D, PACK], BF16, align_bytes=64)
         v_codes = keep.tile([P, HEADS * D], U32, align_bytes=64)
@@ -121,16 +130,21 @@ def tile_chunkedattention_pa_kernel(tc, q, k_means, v_means, intra, wo, bo, out)
         wo_codes = keep.tile([P, GROUPS, E], U32, align_bytes=64)
         wo_scales = keep.tile([P, GROUPS, E], U8, align_bytes=64)
 
+        wo_ps = {}
+
+        def turn_wo(a):
+            wo_ps[a] = out_ps.tile([P, GROUPS * PACK, P], BF16, tag="out", name="wo_ps")
+            for b in range(GROUPS * PACK):
+                nc.tensor.transpose(wo_ps[a][:, b, :], wo_sb[:, a, b * P : (b + 1) * P], ident[:])
+
+        def group_wo(a):
+            copy = nc.scalar.copy if a % 2 == 0 else nc.vector.tensor_copy
+            copy(
+                out=wo_grouped[:, :, a * P : (a + 1) * P, :],
+                in_=wo_ps[a][:].rearrange("p (g t) o -> p g o t", t=PACK),
+            )
+
         def quantise_wo():
-            for a in range(E // P):
-                wo_ps = turn_ps.tile([P, GROUPS * PACK, P], BF16, tag="turn")
-                for b in range(GROUPS * PACK):
-                    nc.tensor.transpose(wo_ps[:, b, :], wo_sb[:, a, b * P : (b + 1) * P], ident[:])
-                copy = nc.scalar.copy if a % 2 == 0 else nc.vector.tensor_copy
-                copy(
-                    out=wo_grouped[:, :, a * P : (a + 1) * P, :],
-                    in_=wo_ps[:].rearrange("p (g t) o -> p g o t", t=PACK),
-                )
             for g in range(GROUPS):
                 nc.vector.quantize_mx(
                     out=wo_codes[:, g, :].bitcast(FP8X4),
@@ -138,128 +152,181 @@ def tile_chunkedattention_pa_kernel(tc, q, k_means, v_means, intra, wo, bo, out)
                     in_=wo_grouped[:, g].rearrange("p o t -> p (o t)"),
                 )
 
-        q_t = {}
-        sums = {}
-        over_sum = {}
-        fused = {}
-        i_ps = {}
+        q_ps, q_t, s_ps, minus_s, shift, sums = {}, {}, {}, {}, {}, {}
+        e_ps, e_codes, e_scales, i_ps, over_sum, fused = {}, {}, {}, {}, {}, {}
+        f_ps, f_grouped, f_codes, f_scales, o_ps = {}, {}, {}, {}, {}
 
         def turn_q(i):
-            q_ps = turn_ps.tile([P, HEADS, P], BF16, tag="turn")
+            q_ps[i] = turn_ps.tile([P, HEADS, P], BF16, tag="turn", name="q_ps")
             for h in range(HEADS):
-                nc.tensor.transpose(q_ps[:, h, :], q_sb[i][:, h, :], ident[:])
+                nc.tensor.transpose(q_ps[i][:, h, :], q_sb[i][:, h, :], ident[:])
+
+        def keep_q(i):
             q_t[i] = work.tile([P, HEADS, P], BF16, name="q_t")
-            nc.scalar.copy(out=q_t[i][:], in_=q_ps[:])
+            nc.scalar.copy(out=q_t[i][:], in_=q_ps[i][:])
             sums[i] = small.tile([P, HEADS], F32, name="sums")
 
-        def softmax(i, a):
-            width = TILE_CHUNKS * (i + 1)
-            for h in (2 * a, 2 * a + 1):
-                s_ps = score_ps.tile([P, CHUNKS], F32)
-                nc.tensor.matmul(s_ps[:, 0:width], lhsT=q_t[i][:, h, :], rhs=k_t[:, h, 0:width], start=True, stop=False)
-                nc.tensor.matmul(s_ps[:, width - TILE_CHUNKS : width], lhsT=ident[:], rhs=mask[:], start=False, stop=True)
-                top = small.tile([P, 1], F32)
-                nc.vector.tensor_reduce(out=top[:], in_=s_ps[:, 0:width], axis=AXIS.X, op=ALU.max)
-                shift = small.tile([P, 1], F32)
-                nc.vector.tensor_scalar_mul(out=shift[:], in0=top[:], scalar1=-SCALE)
-                nc.scalar.activation(
-                    out=e_sb[(i % SETS) * HEADS + h][:, 0:width],
-                    in_=s_ps[:, 0:width],
-                    func=ACT.Exp,
-                    bias=shift[:],
-                    scale=SCALE,
-                    accum_out=sums[i][:, h : h + 1],
-                )
+        def width(i):
+            return TILE_CHUNKS * (i + 1)
 
-        def attend(i, a):
-            blocks = i // PACK + 1
-            if a == 0:
-                over_sum[i] = small.tile([P, HEADS], F32, name="over_sum")
-                nc.vector.reciprocal(out=over_sum[i][:], in_=sums[i][:])
-                fused[i] = work.tile([P, HEADS, D], BF16, name="fused")
-            if a % 2 == 0:
-                i_ps[i] = inter_ps.tile([P, PACK, D], F32, name="i_ps")
-            grouped = e_grouped[(i % SETS) * PAIRS + a]
-            e_ps = turn_ps.tile([P, 2, PACK, P], BF16, tag="turn")
+        def score(n):
+            i, h = divmod(n, HEADS)
+            s_ps[n] = score_ps.tile([P, CHUNKS], F32, name="s_ps")
+            nc.tensor.matmul(s_ps[n][:, 0 : width(i)], lhsT=q_t[i][:, h, :], rhs=k_t[:, h, 0 : width(i)], start=True, stop=False)
+            nc.tensor.matmul(s_ps[n][:, width(i) - TILE_CHUNKS : width(i)], lhsT=ident[:], rhs=mask[:], start=False, stop=True)
+
+        def top(n):
+            i = n // HEADS
+            minus_s[n] = work.tile([P, CHUNKS], F32, name="minus_s")
+            shift[n] = small.tile([P, 1], F32, name="shift")
+            nc.vector.tensor_scalar(
+                out=minus_s[n][:, 0 : width(i)],
+                in0=s_ps[n][:, 0 : width(i)],
+                scalar1=-SCALE,
+                scalar2=None,
+                op0=ALU.mult,
+                op1=ALU.min,
+                accum_out=shift[n][:],
+            )
+
+        def exponent(n):
+            i, h = divmod(n, HEADS)
+            nc.scalar.activation(
+                out=e_sb[h][:, 0 : width(i)],
+                in_=minus_s[n][:, 0 : width(i)],
+                func=ACT.Exp,
+                bias=shift[n][:],
+                scale=-1.0,
+                accum_out=sums[i][:, h : h + 1],
+            )
+
+        def blocks(m):
+            return m // PAIRS // PACK + 1
+
+        def turn_e(m):
+            a = m % PAIRS
+            e_ps[m] = turn_ps.tile([P, 2, PACK, P], BF16, tag="turn", name="e_ps")
             for b in range(2):
-                for t in range(blocks):
-                    nc.tensor.transpose(e_ps[:, b, t, :], e_sb[(i % SETS) * HEADS + 2 * a + b][:, t * P : (t + 1) * P], ident[:])
+                for t in range(blocks(m)):
+                    nc.tensor.transpose(e_ps[m][:, b, t, :], e_sb[2 * a + b][:, t * P : (t + 1) * P], ident[:])
+
+        def group_e(m):
             nc.scalar.copy(
-                out=grouped[:, :, :, 0:blocks],
-                in_=e_ps[:, :, 0:blocks, :].rearrange("p b t r -> p b r t"),
+                out=e_grouped[m % PAIRS][:, :, :, 0 : blocks(m)],
+                in_=e_ps[m][:, :, 0 : blocks(m), :].rearrange("p b t r -> p b r t"),
             )
-            e_codes = work.tile([P, 2, P], U32, align_bytes=64)
-            e_scales = work.tile([P, 2, P], U8, align_bytes=64)
+
+        def quantise_e(m):
+            e_codes[m] = work.tile([P, 2, P], U32, align_bytes=64, name="e_codes")
+            e_scales[m] = work.tile([P, 2, P], U8, align_bytes=64, name="e_scales")
             nc.vector.quantize_mx(
-                out=e_codes[:].rearrange("p b r -> p (b r)").bitcast(FP8X4),
-                scales=e_scales[:].rearrange("p b r -> p (b r)"),
-                in_=grouped[:].rearrange("p b r t -> p (b r t)"),
+                out=e_codes[m][:].rearrange("p b r -> p (b r)").bitcast(FP8X4),
+                scales=e_scales[m][:].rearrange("p b r -> p (b r)"),
+                in_=e_grouped[m % PAIRS][:].rearrange("p b r t -> p (b r t)"),
             )
-            for b in range(2):
-                h = 2 * a + b
+
+        def attend(x):
+            i_ps[x] = inter_ps.tile([P, PACK, D], F32, name="i_ps")
+            for t in range(PACK):
+                h = PACK * (x % GROUPS) + t
+                m = 2 * x + t // 2
                 nc.tensor.matmul_mx(
-                    out=i_ps[i][:, h % PACK, :],
-                    lhsT=e_codes[:, b, :].bitcast(FP8X4),
-                    lhsT_scale=e_scales[:, b, :],
+                    out=i_ps[x][:, t, :],
+                    lhsT=e_codes[m][:, t % 2, :].bitcast(FP8X4),
+                    lhsT_scale=e_scales[m][:, t % 2, :],
                     rhs=v_codes[:, h * D : (h + 1) * D].bitcast(FP8X4),
                     rhs_scale=v_scales[:, h * D : (h + 1) * D],
                     start=True,
                     stop=True,
                 )
-            for b in range(2):
-                h = 2 * a + b
+
+        def fuse(x):
+            i, g = divmod(x, GROUPS)
+            if g == 0:
+                over_sum[i] = small.tile([P, HEADS], F32, name="over_sum")
+                nc.vector.reciprocal(out=over_sum[i][:], in_=sums[i][:])
+                fused[i] = work.tile([P, HEADS, D], BF16, name="fused")
+            for t in range(PACK):
+                h = PACK * g + t
                 nc.vector.scalar_tensor_tensor(
                     out=fused[i][:, h, :],
-                    in0=i_ps[i][:, h % PACK, :],
+                    in0=i_ps[x][:, t, :],
                     scalar=over_sum[i][:, h : h + 1],
                     in1=intra_sb[i][:, h, :],
                     op0=ALU.mult,
                     op1=ALU.add,
                 )
 
-        def project(i):
-            f_ps = turn_ps.tile([P, HEADS, P], BF16, tag="turn")
+        def turn_f(i):
+            f_ps[i] = turn_ps.tile([P, HEADS, P], BF16, tag="turn", name="f_ps")
             for h in range(HEADS):
-                nc.tensor.transpose(f_ps[:, h, :], fused[i][:, h, :], ident[:])
-            f_grouped = work.tile([P, GROUPS, P, PACK], BF16, align_bytes=64)
-            nc.scalar.copy(out=f_grouped[:], in_=f_ps[:].rearrange("p (g t) r -> p g r t", t=PACK))
-            f_codes = work.tile([P, GROUPS, P], U32, align_bytes=64)
-            f_scales = work.tile([P, GROUPS, P], U8, align_bytes=64)
-            nc.vector.quantize_mx(
-                out=f_codes[:].rearrange("p g r -> p (g r)").bitcast(FP8X4),
-                scales=f_scales[:].rearrange("p g r -> p (g r)"),
-                in_=f_grouped[:].rearrange("p g r t -> p (g r t)"),
-            )
-            result = store.tile([P, E], F32)
-            for n in range(E // HALF):
-                cols = slice(n * HALF, (n + 1) * HALF)
-                o_ps = out_ps.tile([P, HALF], F32)
-                for g in range(GROUPS):
-                    nc.tensor.matmul_mx(
-                        out=o_ps[:],
-                        lhsT=f_codes[:, g, :].bitcast(FP8X4),
-                        lhsT_scale=f_scales[:, g, :],
-                        rhs=wo_codes[:, g, cols].bitcast(FP8X4),
-                        rhs_scale=wo_scales[:, g, cols],
-                        start=(g == 0),
-                        stop=(g == GROUPS - 1),
-                    )
-                nc.vector.tensor_tensor(out=result[:, cols], in0=o_ps[:], in1=bias[:, cols], op=ALU.add)
-            nc.sync.dma_start(out=out_rows[i * P : (i + 1) * P, :], in_=result[:])
+                nc.tensor.transpose(f_ps[i][:, h, :], fused[i][:, h, :], ident[:])
 
-        turn_k(0)
-        turn_q(0)
-        quantise_v()
-        quantise_wo()
-        for n in range(TILES + 2):
-            if 0 <= n - 2:
-                project(n - 2)
-            if n + 1 < TILES:
-                if (n + 1) % PACK == 0:
-                    turn_k((n + 1) // PACK)
-                turn_q(n + 1)
-            for a in range(PAIRS):
-                if 0 <= n - 1 < TILES:
-                    attend(n - 1, a)
-                if n < TILES:
-                    softmax(n, a)
+        def group_f(i):
+            f_grouped[i] = work.tile([P, GROUPS, P, PACK], BF16, align_bytes=64, name="f_grouped")
+            nc.scalar.copy(out=f_grouped[i][:], in_=f_ps[i][:].rearrange("p (g t) r -> p g r t", t=PACK))
+
+        def quantise_f(i):
+            f_codes[i] = work.tile([P, GROUPS, P], U32, align_bytes=64, name="f_codes")
+            f_scales[i] = work.tile([P, GROUPS, P], U8, align_bytes=64, name="f_scales")
+            nc.vector.quantize_mx(
+                out=f_codes[i][:].rearrange("p g r -> p (g r)").bitcast(FP8X4),
+                scales=f_scales[i][:].rearrange("p g r -> p (g r)"),
+                in_=f_grouped[i][:].rearrange("p g r t -> p (g r t)"),
+            )
+
+        result = {}
+
+        def project(y):
+            i, c = divmod(y, E // HALF)
+            o_ps[y] = out_ps.tile([P, HALF], F32, tag="out", name="o_ps")
+            for g in range(GROUPS):
+                nc.tensor.matmul_mx(
+                    out=o_ps[y][:],
+                    lhsT=f_codes[i][:, g, :].bitcast(FP8X4),
+                    lhsT_scale=f_scales[i][:, g, :],
+                    rhs=wo_codes[:, g, c * HALF : (c + 1) * HALF].bitcast(FP8X4),
+                    rhs_scale=wo_scales[:, g, c * HALF : (c + 1) * HALF],
+                    start=(g == 0),
+                    stop=(g == GROUPS - 1),
+                )
+
+        def finish(y):
+            i, c = divmod(y, E // HALF)
+            cols = slice(c * HALF, (c + 1) * HALF)
+            if c == 0:
+                result[i] = store.tile([P, E], F32, name="result")
+            nc.vector.tensor_tensor(out=result[i][:, cols], in0=o_ps[y][:], in1=bias[:, cols], op=ALU.add)
+            if c == E // HALF - 1:
+                nc.sync.dma_start(out=out_rows[i * P : (i + 1) * P, :], in_=result[i][:])
+
+        def run(step, tick, first, period, count):
+            x, rest = divmod(tick - first, period)
+            if rest == 0 and 0 <= x < count:
+                step(x)
+
+        n_heads, n_pairs, n_fours, n_halves = TILES * HEADS, TILES * PAIRS, TILES * GROUPS, TILES * E // HALF
+        for tick in range(-9, n_heads + 40):
+            run(finish, tick, 42, 4, n_halves)
+            run(quantise_f, tick, 37, HEADS, TILES)
+            run(group_f, tick, 35, HEADS, TILES)
+            run(fuse, tick, 18, 4, n_fours)
+            run(quantise_e, tick, 12, 2, n_pairs)
+            run(group_e, tick, 10, 2, n_pairs)
+            run(exponent, tick, 4, 1, n_heads)
+            run(top, tick, 2, 1, n_heads)
+            run(keep_q, tick, -3, HEADS, TILES)
+            run(keep_k, tick, -7, HEADS * PACK, PACK)
+            run(group_wo, tick, 8, 4, E // P)
+            if tick == 10:
+                quantise_v()
+            if tick == 38:
+                quantise_wo()
+            run(project, tick, 40, 4, n_halves)
+            run(attend, tick, 16, 4, n_fours)
+            run(turn_wo, tick, 6, 4, E // P)
+            run(turn_f, tick, 33, HEADS, TILES)
+            run(turn_e, tick, 8, 2, n_pairs)
+            run(turn_q, tick, -5, HEADS, TILES)
+            run(turn_k, tick, -9, HEADS * PACK, PACK)
+            run(score, tick, 0, 1, n_heads)

@@ -240,11 +240,13 @@ def tile_chunkedattention_pa_kernel(tc, q, k_means, v_means, intra, wo, bo, out)
                     stop=True,
                 )
 
+        def invert(i):
+            over_sum[i] = small.tile([P, HEADS], F32, name="over_sum")
+            nc.vector.reciprocal(out=over_sum[i][:], in_=sums[i][:])
+
         def fuse(x):
             i, g = divmod(x, GROUPS)
             if g == 0:
-                over_sum[i] = small.tile([P, HEADS], F32, name="over_sum")
-                nc.vector.reciprocal(out=over_sum[i][:], in_=sums[i][:])
                 fused[i] = work.tile([P, HEADS, D], BF16, name="fused")
             for t in range(PACK):
                 h = PACK * g + t
@@ -263,8 +265,9 @@ def tile_chunkedattention_pa_kernel(tc, q, k_means, v_means, intra, wo, bo, out)
                 nc.tensor.transpose(f_ps[i][:, h, :], fused[i][:, h, :], ident[:])
 
         def group_f(i):
+            copy = nc.scalar.copy if i < TILES // 2 else nc.vector.tensor_copy
             f_grouped[i] = work.tile([P, GROUPS, P, PACK], BF16, align_bytes=64, name="f_grouped")
-            nc.scalar.copy(out=f_grouped[i][:], in_=f_ps[i][:].rearrange("p (g t) r -> p g r t", t=PACK))
+            copy(out=f_grouped[i][:], in_=f_ps[i][:].rearrange("p (g t) r -> p g r t", t=PACK))
 
         def quantise_f(i):
             f_codes[i] = work.tile([P, GROUPS, P], U32, align_bytes=64, name="f_codes")
@@ -311,6 +314,7 @@ def tile_chunkedattention_pa_kernel(tc, q, k_means, v_means, intra, wo, bo, out)
             run(quantise_f, tick, 37, HEADS, TILES)
             run(group_f, tick, 35, HEADS, TILES)
             run(fuse, tick, 18, 4, n_fours)
+            run(invert, tick, 14, HEADS, TILES)
             run(quantise_e, tick, 12, 2, n_pairs)
             run(group_e, tick, 10, 2, n_pairs)
             run(exponent, tick, 4, 1, n_heads)

@@ -45,11 +45,10 @@ def tile_chunkedattention_pa_kernel(tc, q, k_means, v_means, intra, wo, bo, out)
         keep = ctx.enter_context(tc.tile_pool(name="keep", bufs=1))
         work = ctx.enter_context(tc.tile_pool(name="work", bufs=4))
         small = ctx.enter_context(tc.tile_pool(name="small", bufs=6))
-        store = ctx.enter_context(tc.tile_pool(name="store", bufs=3))
+        store = ctx.enter_context(tc.tile_pool(name="store", bufs=4))
         turn_ps = ctx.enter_context(tc.psum_pool(name="turn_ps", bufs=3))
         score_ps = ctx.enter_context(tc.psum_pool(name="score_ps", bufs=3))
-        inter_ps = ctx.enter_context(tc.psum_pool(name="inter_ps", bufs=1))
-        out_ps = ctx.enter_context(tc.psum_pool(name="out_ps", bufs=1))
+        mx_ps = ctx.enter_context(tc.psum_pool(name="mx_ps", bufs=2))
 
         k_sb = keep.tile([P, PACK, HEADS, D], BF16)
         v_sb = keep.tile([P, PACK, HEADS, D], BF16)
@@ -133,7 +132,7 @@ def tile_chunkedattention_pa_kernel(tc, q, k_means, v_means, intra, wo, bo, out)
         wo_ps = {}
 
         def turn_wo(a):
-            wo_ps[a] = out_ps.tile([P, GROUPS * PACK, P], BF16, tag="out", name="wo_ps")
+            wo_ps[a] = mx_ps.tile([P, GROUPS * PACK, P], BF16, tag="mx", name="wo_ps")
             for b in range(GROUPS * PACK):
                 nc.tensor.transpose(wo_ps[a][:, b, :], wo_sb[:, a, b * P : (b + 1) * P], ident[:])
 
@@ -226,7 +225,7 @@ def tile_chunkedattention_pa_kernel(tc, q, k_means, v_means, intra, wo, bo, out)
             )
 
         def attend(x):
-            i_ps[x] = inter_ps.tile([P, PACK, D], F32, name="i_ps")
+            i_ps[x] = mx_ps.tile([P, PACK, D], F32, tag="mx", name="i_ps")
             for t in range(PACK):
                 h = PACK * (x % GROUPS) + t
                 m = 2 * x + t // 2
@@ -265,7 +264,7 @@ def tile_chunkedattention_pa_kernel(tc, q, k_means, v_means, intra, wo, bo, out)
                 nc.tensor.transpose(f_ps[i][:, h, :], fused[i][:, h, :], ident[:])
 
         def group_f(i):
-            copy = nc.scalar.copy if i < TILES // 2 else nc.vector.tensor_copy
+            copy = nc.vector.tensor_copy if 8 <= i <= 12 else nc.scalar.copy
             f_grouped[i] = work.tile([P, GROUPS, P, PACK], BF16, align_bytes=64, name="f_grouped")
             copy(out=f_grouped[i][:], in_=f_ps[i][:].rearrange("p (g t) r -> p g r t", t=PACK))
 
@@ -278,11 +277,9 @@ def tile_chunkedattention_pa_kernel(tc, q, k_means, v_means, intra, wo, bo, out)
                 in_=f_grouped[i][:].rearrange("p g r t -> p (g r t)"),
             )
 
-        result = {}
-
         def project(y):
             i, c = divmod(y, E // HALF)
-            o_ps[y] = out_ps.tile([P, HALF], F32, tag="out", name="o_ps")
+            o_ps[y] = mx_ps.tile([P, HALF], F32, tag="mx", name="o_ps")
             for g in range(GROUPS):
                 nc.tensor.matmul_mx(
                     out=o_ps[y][:],
@@ -297,11 +294,9 @@ def tile_chunkedattention_pa_kernel(tc, q, k_means, v_means, intra, wo, bo, out)
         def finish(y):
             i, c = divmod(y, E // HALF)
             cols = slice(c * HALF, (c + 1) * HALF)
-            if c == 0:
-                result[i] = store.tile([P, E], F32, name="result")
-            nc.vector.tensor_tensor(out=result[i][:, cols], in0=o_ps[y][:], in1=bias[:, cols], op=ALU.add)
-            if c == E // HALF - 1:
-                nc.sync.dma_start(out=out_rows[i * P : (i + 1) * P, :], in_=result[i][:])
+            result = store.tile([P, HALF], F32)
+            nc.vector.tensor_tensor(out=result[:], in0=o_ps[y][:], in1=bias[:, cols], op=ALU.add)
+            nc.sync.dma_start(out=out_rows[i * P : (i + 1) * P, cols], in_=result[:])
 
         def run(step, tick, first, period, count):
             x, rest = divmod(tick - first, period)
@@ -309,8 +304,8 @@ def tile_chunkedattention_pa_kernel(tc, q, k_means, v_means, intra, wo, bo, out)
                 step(x)
 
         n_heads, n_pairs, n_fours, n_halves = TILES * HEADS, TILES * PAIRS, TILES * GROUPS, TILES * E // HALF
-        for tick in range(-9, n_heads + 40):
-            run(finish, tick, 42, 4, n_halves)
+        for tick in range(-9, n_heads + 42):
+            run(finish, tick, 44, 4, n_halves)
             run(quantise_f, tick, 37, HEADS, TILES)
             run(group_f, tick, 35, HEADS, TILES)
             run(fuse, tick, 18, 4, n_fours)
@@ -326,7 +321,7 @@ def tile_chunkedattention_pa_kernel(tc, q, k_means, v_means, intra, wo, bo, out)
                 quantise_v()
             if tick == 38:
                 quantise_wo()
-            run(project, tick, 40, 4, n_halves)
+            run(project, tick, 42, 4, n_halves)
             run(attend, tick, 16, 4, n_fours)
             run(turn_wo, tick, 6, 4, E // P)
             run(turn_f, tick, 33, HEADS, TILES)

@@ -37,7 +37,7 @@ def tile_chunkedattention_pa_kernel(tc, q, k_means, v_means, intra, wo, bo, out)
     q_rows = q.rearrange("b h c t d -> (b h) (c t) d")
     intra_rows = intra.rearrange("b h c t d -> (b h) (c t) d")
     k_blocks = k_means.rearrange("b h (t p) d -> t p (b h) d", p=P)
-    v_blocks = v_means.rearrange("b h (t p) d -> t p (b h) d", p=P)
+    v_blocks = v_means.rearrange("b h (u p e) d -> u e p (b h) d", p=P, e=2)
     out_rows = out.rearrange("b s o -> (b s) o")
 
     with ExitStack() as ctx:
@@ -65,7 +65,7 @@ def tile_chunkedattention_pa_kernel(tc, q, k_means, v_means, intra, wo, bo, out)
         load_rows(q_sb, q_rows, 0)
         load_rows(q_sb, q_rows, 1)
         for t in range(PACK):
-            nc.sync.dma_start(out=v_sb[:, t], in_=v_blocks[t])
+            nc.sync.dma_start(out=v_sb[:, t], in_=v_blocks[t // 2, t % 2])
         for i in range(TILES):
             if i < PACK:
                 for a in (2 * i, 2 * i + 1):
@@ -80,6 +80,8 @@ def tile_chunkedattention_pa_kernel(tc, q, k_means, v_means, intra, wo, bo, out)
 
         ident = keep.tile([P, P], BF16)
         make_identity(nc, ident[:])
+        ident_f32 = keep.tile([P, P], F32)
+        make_identity(nc, ident_f32[:])
         mask_f32 = keep.tile([P, TILE_CHUNKS], F32)
         nc.gpsimd.memset(mask_f32[:], 0.0)
         nc.gpsimd.affine_select(
@@ -111,7 +113,7 @@ def tile_chunkedattention_pa_kernel(tc, q, k_means, v_means, intra, wo, bo, out)
                 nc.tensor.transpose(k_ps[t][:, h, :], k_sb[:, t, h, :], ident[:])
 
         def keep_k(t):
-            nc.vector.tensor_copy(out=k_t[:, :, t * P : (t + 1) * P], in_=k_ps[t][:])
+            nc.scalar.copy(out=k_t[:, :, t * P : (t + 1) * P], in_=k_ps[t][:])
 
         v_grouped = keep.tile([P, HEADS * D, PACK], BF16, align_bytes=64)
         v_codes = keep.tile([P, HEADS * D], U32, align_bytes=64)
@@ -132,15 +134,14 @@ def tile_chunkedattention_pa_kernel(tc, q, k_means, v_means, intra, wo, bo, out)
         wo_ps = {}
 
         def turn_wo(a):
-            wo_ps[a] = mx_ps.tile([P, GROUPS * PACK, P], BF16, tag="mx", name="wo_ps")
-            for b in range(GROUPS * PACK):
-                nc.tensor.transpose(wo_ps[a][:, b, :], wo_sb[:, a, b * P : (b + 1) * P], ident[:])
+            wo_ps[a] = mx_ps.tile([P, GROUPS * 2, P], F32, tag="mx", name="wo_ps")
+            for b in range(GROUPS * 2):
+                nc.tensor.transpose(wo_ps[a][:, b, :], wo_sb[:, a, :].bitcast(F32)[:, b * P : (b + 1) * P], ident_f32[:])
 
         def group_wo(a):
-            copy = nc.scalar.copy if a % 2 == 0 else nc.vector.tensor_copy
-            copy(
-                out=wo_grouped[:, :, a * P : (a + 1) * P, :],
-                in_=wo_ps[a][:].rearrange("p (g t) o -> p g o t", t=PACK),
+            nc.scalar.copy(
+                out=wo_grouped[:, :, a * P : (a + 1) * P, :].bitcast(F32),
+                in_=wo_ps[a][:].rearrange("p (g u) o -> p g o u", u=2),
             )
 
         def quantise_wo():
@@ -199,20 +200,20 @@ def tile_chunkedattention_pa_kernel(tc, q, k_means, v_means, intra, wo, bo, out)
                 accum_out=sums[i][:, h : h + 1],
             )
 
-        def blocks(m):
-            return m // PAIRS // PACK + 1
+        def halves(m):
+            return m // PAIRS // (TILES // 2) + 1
 
         def turn_e(m):
             a = m % PAIRS
-            e_ps[m] = turn_ps.tile([P, 2, PACK, P], BF16, tag="turn", name="e_ps")
+            e_ps[m] = turn_ps.tile([P, 2, 2, P], F32, tag="turn", name="e_ps")
             for b in range(2):
-                for t in range(blocks(m)):
-                    nc.tensor.transpose(e_ps[m][:, b, t, :], e_sb[2 * a + b][:, t * P : (t + 1) * P], ident[:])
+                for u in range(halves(m)):
+                    nc.tensor.transpose(e_ps[m][:, b, u, :], e_sb[2 * a + b][:].bitcast(F32)[:, u * P : (u + 1) * P], ident_f32[:])
 
         def group_e(m):
             nc.scalar.copy(
-                out=e_grouped[m % PAIRS][:, :, :, 0 : blocks(m)],
-                in_=e_ps[m][:, :, 0 : blocks(m), :].rearrange("p b t r -> p b r t"),
+                out=e_grouped[m % PAIRS][:].bitcast(F32)[:, :, :, 0 : halves(m)],
+                in_=e_ps[m][:, :, 0 : halves(m), :].rearrange("p b u r -> p b r u"),
             )
 
         def quantise_e(m):
@@ -259,14 +260,14 @@ def tile_chunkedattention_pa_kernel(tc, q, k_means, v_means, intra, wo, bo, out)
                 )
 
         def turn_f(i):
-            f_ps[i] = turn_ps.tile([P, HEADS, P], BF16, tag="turn", name="f_ps")
-            for h in range(HEADS):
-                nc.tensor.transpose(f_ps[i][:, h, :], fused[i][:, h, :], ident[:])
+            f_ps[i] = turn_ps.tile([P, GROUPS * 2, P], F32, tag="turn", name="f_ps")
+            words = fused[i][:].rearrange("p h d -> p (h d)").bitcast(F32)
+            for b in range(GROUPS * 2):
+                nc.tensor.transpose(f_ps[i][:, b, :], words[:, b * P : (b + 1) * P], ident_f32[:])
 
         def group_f(i):
-            copy = nc.vector.tensor_copy if 8 <= i <= 12 else nc.scalar.copy
             f_grouped[i] = work.tile([P, GROUPS, P, PACK], BF16, align_bytes=64, name="f_grouped")
-            copy(out=f_grouped[i][:], in_=f_ps[i][:].rearrange("p (g t) r -> p g r t", t=PACK))
+            nc.scalar.copy(out=f_grouped[i][:].bitcast(F32), in_=f_ps[i][:].rearrange("p (g u) r -> p g r u", u=2))
 
         def quantise_f(i):
             f_codes[i] = work.tile([P, GROUPS, P], U32, align_bytes=64, name="f_codes")

@@ -97,11 +97,12 @@ def tile_chunkedattention_pa_kernel(tc, q, k_means, v_means, intra, wo, bo, out)
         nc.vector.tensor_copy(out=mask[:], in_=mask_f32[:])
 
         e_sb = [keep.tile([P, CHUNKS], BF16, name="e_sb%d" % n) for n in range(HEADS)]
-        e_grouped = [keep.tile([P, 2, P, PACK], BF16, name="e_grouped%d" % n, align_bytes=64) for n in range(PAIRS)]
         for n in range(HEADS):
             nc.gpsimd.memset(e_sb[n][:], 0.0)
-        for n in range(PAIRS):
-            nc.vector.memset(e_grouped[n][:], 0.0)
+
+        warm = small.tile([P, 1], F32)
+        nc.vector.memset(warm[:], 0.0)
+        nc.scalar.activation(out=warm[:], in_=warm[:], func=ACT.Exp)
 
         k_t = keep.tile([P, HEADS, CHUNKS], BF16)
 
@@ -153,7 +154,7 @@ def tile_chunkedattention_pa_kernel(tc, q, k_means, v_means, intra, wo, bo, out)
                 )
 
         q_ps, q_t, s_ps, minus_s, shift, sums = {}, {}, {}, {}, {}, {}
-        e_ps, e_codes, e_scales, i_ps, over_sum, fused = {}, {}, {}, {}, {}, {}
+        e_ps, e_grouped, e_codes, e_scales, i_ps, over_sum, fused = {}, {}, {}, {}, {}, {}, {}
         f_ps, f_grouped, f_codes, f_scales, o_ps = {}, {}, {}, {}, {}
 
         def turn_q(i):
@@ -200,21 +201,16 @@ def tile_chunkedattention_pa_kernel(tc, q, k_means, v_means, intra, wo, bo, out)
                 accum_out=sums[i][:, h : h + 1],
             )
 
-        def halves(m):
-            return m // PAIRS // (TILES // 2) + 1
-
         def turn_e(m):
             a = m % PAIRS
             e_ps[m] = turn_ps.tile([P, 2, 2, P], F32, tag="turn", name="e_ps")
             for b in range(2):
-                for u in range(halves(m)):
+                for u in range(2):
                     nc.tensor.transpose(e_ps[m][:, b, u, :], e_sb[2 * a + b][:].bitcast(F32)[:, u * P : (u + 1) * P], ident_f32[:])
 
         def group_e(m):
-            nc.scalar.copy(
-                out=e_grouped[m % PAIRS][:].bitcast(F32)[:, :, :, 0 : halves(m)],
-                in_=e_ps[m][:, :, 0 : halves(m), :].rearrange("p b u r -> p b r u"),
-            )
+            e_grouped[m] = work.tile([P, 2, P, PACK], BF16, align_bytes=64, name="e_grouped")
+            nc.scalar.copy(out=e_grouped[m][:].bitcast(F32), in_=e_ps[m][:].rearrange("p b u r -> p b r u"))
 
         def quantise_e(m):
             e_codes[m] = work.tile([P, 2, P], U32, align_bytes=64, name="e_codes")
@@ -222,7 +218,7 @@ def tile_chunkedattention_pa_kernel(tc, q, k_means, v_means, intra, wo, bo, out)
             nc.vector.quantize_mx(
                 out=e_codes[m][:].rearrange("p b r -> p (b r)").bitcast(FP8X4),
                 scales=e_scales[m][:].rearrange("p b r -> p (b r)"),
-                in_=e_grouped[m % PAIRS][:].rearrange("p b r t -> p (b r t)"),
+                in_=e_grouped[m][:].rearrange("p b r t -> p (b r t)"),
             )
 
         def attend(x):

@@ -6,6 +6,7 @@ from concourse.masks import make_identity
 
 BF16 = mybir.dt.bfloat16
 F32 = mybir.dt.float32
+I32 = mybir.dt.int32
 U32 = mybir.dt.uint32
 U8 = mybir.dt.uint8
 FP8X4 = mybir.dt.float8_e4m3fn_x4
@@ -26,10 +27,17 @@ TILE_CHUNKS = P // PLACES
 GROUPS = E // (P * PACK)
 HALF = 512
 SCALE = 1.0 / math.sqrt(D)
-PAIRS = HEADS // 2
 MASKED = -1.0e30
 
 FLOPS = 2 * HEADS * TOKENS * CHUNKS * D * 2 + 2 * TOKENS * E * E
+
+
+def width(i):
+    return TILE_CHUNKS * (i + 1)
+
+
+def share(i):
+    return 4 if width(i) <= 128 else 2 if width(i) <= 256 else 1
 
 
 def tile_chunkedattention_pa_kernel(tc, q, k_means, v_means, intra, wo, bo, out):
@@ -51,32 +59,50 @@ def tile_chunkedattention_pa_kernel(tc, q, k_means, v_means, intra, wo, bo, out)
         mx_ps = ctx.enter_context(tc.psum_pool(name="mx_ps", bufs=2))
 
         k_sb = keep.tile([P, PACK, HEADS, D], BF16)
-        v_sb = keep.tile([P, PACK, HEADS, D], BF16)
         wo_sb = keep.tile([P, E // P, E], BF16)
         bias = keep.tile([P, E], BF16)
         q_sb = [keep.tile([P, HEADS, D], BF16, name="q_sb%d" % i) for i in range(TILES)]
         intra_sb = [keep.tile([P, HEADS, D], BF16, name="intra_sb%d" % i) for i in range(TILES)]
+        v_sb = {
+            1: keep.tile([P, PACK, HEADS, D], BF16, name="v_sb1"),
+            2: keep.tile([P, HEADS // 2, PACK, D], BF16, name="v_sb2"),
+            4: keep.tile([P, HEADS // 4, PACK, D], BF16, name="v_sb4"),
+        }
 
         def load_rows(tiles, rows, i):
             nc.sync.dma_start(out=tiles[i][:], in_=rows[:, i * P : (i + 1) * P, :].rearrange("h p d -> p h d"))
+
+        def load_v_shared(n):
+            rows = P // n
+            heads = v_means.rearrange("b (a s) j d -> s (b a) j d", s=n)
+            for s in range(n):
+                nc.sync.dma_start(
+                    out=v_sb[n][s * rows : (s + 1) * rows],
+                    in_=heads[s, :, 0 : rows * PACK, :].rearrange("a (p t) d -> p a t d", t=PACK),
+                )
 
         wo_blocks = wo.rearrange("(a p) k -> a p k", p=P)
         nc.sync.dma_start(out=k_sb[:, 0], in_=k_blocks[0])
         load_rows(q_sb, q_rows, 0)
         load_rows(q_sb, q_rows, 1)
-        for t in range(PACK):
-            nc.sync.dma_start(out=v_sb[:, t], in_=v_blocks[t // 2, t % 2])
-        for i in range(TILES):
-            if i < PACK:
-                for a in (2 * i, 2 * i + 1):
-                    nc.sync.dma_start(out=wo_sb[:, a, :], in_=wo_blocks[a])
-            if i + 2 < TILES:
-                load_rows(q_sb, q_rows, i + 2)
-            load_rows(intra_sb, intra_rows, i)
-            if i % PACK == 0 and i // PACK + 1 < PACK:
+        load_v_shared(4)
+        load_rows(intra_sb, intra_rows, 0)
+        for a in range(E // P):
+            nc.sync.dma_start(out=wo_sb[:, a, :], in_=wo_blocks[a])
+            if a == 3:
+                load_rows(q_sb, q_rows, 2)
+        load_rows(intra_sb, intra_rows, 1)
+        nc.sync.dma_start(out=bias[:], in_=bo.partition_broadcast(P))
+        load_v_shared(2)
+        for i in range(3, TILES):
+            load_rows(q_sb, q_rows, i)
+            load_rows(intra_sb, intra_rows, i - 1)
+            if i % PACK == 3 and i // PACK + 1 < PACK:
                 nc.sync.dma_start(out=k_sb[:, i // PACK + 1], in_=k_blocks[i // PACK + 1])
-            if i == PACK:
-                nc.sync.dma_start(out=bias[:], in_=bo.partition_broadcast(P))
+            if i == 4:
+                for t in range(PACK):
+                    nc.sync.dma_start(out=v_sb[1][:, t], in_=v_blocks[t // 2, t % 2])
+        load_rows(intra_sb, intra_rows, TILES - 1)
 
         ident = keep.tile([P, P], BF16)
         make_identity(nc, ident[:])
@@ -96,9 +122,21 @@ def tile_chunkedattention_pa_kernel(tc, q, k_means, v_means, intra, wo, bo, out)
         mask = keep.tile([P, TILE_CHUNKS], BF16)
         nc.vector.tensor_copy(out=mask[:], in_=mask_f32[:])
 
-        e_sb = [keep.tile([P, CHUNKS], BF16, name="e_sb%d" % n) for n in range(HEADS)]
-        for n in range(HEADS):
-            nc.gpsimd.memset(e_sb[n][:], 0.0)
+        e_sets = {4: 4, 2: 4, 1: 8}
+        e_sb, v_codes = {}, {}
+        for n in (4, 2, 1):
+            e_sb[n] = [keep.tile([P, n, CHUNKS // n], BF16, name="e_sb%d_%d" % (n, r)) for r in range(e_sets[n])]
+            v_codes[n] = keep.tile([P, HEADS, D], U32, align_bytes=64, name="v_codes%d" % n)
+
+        def zero_e(engine, n, r):
+            engine.memset(e_sb[n][r][:].rearrange("p n j -> p (n j)").bitcast(F32), 0.0)
+
+        def zero_v(engine, n):
+            engine.memset(v_codes[n][:], 0)
+
+        for r in range(e_sets[4]):
+            zero_e(nc.vector, 4, r)
+        zero_v(nc.vector, 4)
 
         warm = small.tile([P, 1], F32)
         nc.vector.memset(warm[:], 0.0)
@@ -116,16 +154,40 @@ def tile_chunkedattention_pa_kernel(tc, q, k_means, v_means, intra, wo, bo, out)
         def keep_k(t):
             nc.scalar.copy(out=k_t[:, :, t * P : (t + 1) * P], in_=k_ps[t][:])
 
-        v_grouped = keep.tile([P, HEADS * D, PACK], BF16, align_bytes=64)
-        v_codes = keep.tile([P, HEADS * D], U32, align_bytes=64)
-        v_scales = keep.tile([P, HEADS * D], U8, align_bytes=64)
+        v_grouped = {1: keep.tile([P, HEADS, D, PACK], BF16, align_bytes=64, name="v_grouped1")}
+        v_scales = {1: keep.tile([P, HEADS, D], U8, align_bytes=64, name="v_scales1")}
+        v_dense = {}
+        for n in (2, 4):
+            v_grouped[n] = keep.tile([P, HEADS // n, D, PACK], BF16, align_bytes=64, name="v_grouped%d" % n)
+            v_scales[n] = keep.tile([P, HEADS // n, D], U8, align_bytes=64, name="v_scales%d" % n)
+            v_dense[n] = keep.tile([P, HEADS // n, D], U32, align_bytes=64, name="v_dense%d" % n)
+
+        def group_v_shared(n):
+            nc.vector.tensor_copy(out=v_grouped[n][:], in_=v_sb[n][:].rearrange("p a t d -> p a d t"))
+
+        def quantise_v_shared(n):
+            nc.vector.quantize_mx(
+                out=v_dense[n][:].rearrange("p a d -> p (a d)").bitcast(FP8X4),
+                scales=v_scales[n][:].rearrange("p a d -> p (a d)"),
+                in_=v_grouped[n][:].rearrange("p a d t -> p (a d t)"),
+            )
+
+        def spread_v(n):
+            rows = P // n
+            heads = v_codes[n][:].rearrange("p (a s) d -> p a s d", s=n)
+            for s in range(n):
+                part = slice(s * rows, (s + 1) * rows)
+                nc.vector.tensor_copy(out=heads[part, :, s, :].bitcast(I32), in_=v_dense[n][part].bitcast(I32))
+
+        def group_v(a):
+            heads = slice(2 * a, 2 * a + 2)
+            nc.scalar.copy(out=v_grouped[1][:, heads], in_=v_sb[1][:, :, heads, :].rearrange("p t h d -> p h d t"))
 
         def quantise_v():
-            nc.vector.tensor_copy(out=v_grouped[:], in_=v_sb[:].rearrange("p t h d -> p (h d) t"))
             nc.vector.quantize_mx(
-                out=v_codes[:].bitcast(FP8X4),
-                scales=v_scales[:],
-                in_=v_grouped[:].rearrange("p c t -> p (c t)"),
+                out=v_codes[1][:].rearrange("p h d -> p (h d)").bitcast(FP8X4),
+                scales=v_scales[1][:].rearrange("p h d -> p (h d)"),
+                in_=v_grouped[1][:].rearrange("p h d t -> p (h d t)"),
             )
 
         wo_grouped = keep.tile([P, GROUPS, E, PACK], BF16, align_bytes=64)
@@ -140,20 +202,19 @@ def tile_chunkedattention_pa_kernel(tc, q, k_means, v_means, intra, wo, bo, out)
                 nc.tensor.transpose(wo_ps[a][:, b, :], wo_sb[:, a, :].bitcast(F32)[:, b * P : (b + 1) * P], ident_f32[:])
 
         def group_wo(a):
-            nc.scalar.copy(
+            (nc.vector.tensor_copy if a % 2 == 0 else nc.scalar.copy)(
                 out=wo_grouped[:, :, a * P : (a + 1) * P, :].bitcast(F32),
                 in_=wo_ps[a][:].rearrange("p (g u) o -> p g o u", u=2),
             )
 
-        def quantise_wo():
-            for g in range(GROUPS):
-                nc.vector.quantize_mx(
-                    out=wo_codes[:, g, :].bitcast(FP8X4),
-                    scales=wo_scales[:, g, :],
-                    in_=wo_grouped[:, g].rearrange("p o t -> p (o t)"),
-                )
+        def quantise_wo(g):
+            nc.vector.quantize_mx(
+                out=wo_codes[:, g, :].bitcast(FP8X4),
+                scales=wo_scales[:, g, :],
+                in_=wo_grouped[:, g].rearrange("p o t -> p (o t)"),
+            )
 
-        q_ps, q_t, s_ps, minus_s, shift, sums = {}, {}, {}, {}, {}, {}
+        q_ps, q_t, s_ps, top_s, shift, sums = {}, {}, {}, {}, {}, {}
         e_ps, e_grouped, e_codes, e_scales, i_ps, over_sum, fused = {}, {}, {}, {}, {}, {}, {}
         f_ps, f_grouped, f_codes, f_scales, o_ps = {}, {}, {}, {}, {}
 
@@ -167,71 +228,72 @@ def tile_chunkedattention_pa_kernel(tc, q, k_means, v_means, intra, wo, bo, out)
             nc.scalar.copy(out=q_t[i][:], in_=q_ps[i][:])
             sums[i] = small.tile([P, HEADS], F32, name="sums")
 
-        def width(i):
-            return TILE_CHUNKS * (i + 1)
+        def e_tile(i, h):
+            n = share(i)
+            return e_sb[n][(i * (HEADS // n) + h // n) % e_sets[n]]
 
-        def score(n):
-            i, h = divmod(n, HEADS)
-            s_ps[n] = score_ps.tile([P, CHUNKS], F32, name="s_ps")
-            nc.tensor.matmul(s_ps[n][:, 0 : width(i)], lhsT=q_t[i][:, h, :], rhs=k_t[:, h, 0 : width(i)], start=True, stop=False)
-            nc.tensor.matmul(s_ps[n][:, width(i) - TILE_CHUNKS : width(i)], lhsT=ident[:], rhs=mask[:], start=False, stop=True)
+        def score(i, h0):
+            n, w = share(i), width(i)
+            s_ps[i, h0] = score_ps.tile([P, n, CHUNKS // n], F32, name="s_ps")
+            for b in range(n):
+                bank = s_ps[i, h0][:, b, :]
+                nc.tensor.matmul(bank[:, 0:w], lhsT=q_t[i][:, h0 + b, :], rhs=k_t[:, h0 + b, 0:w], start=True, stop=False)
+                nc.tensor.matmul(bank[:, w - TILE_CHUNKS : w], lhsT=ident[:], rhs=mask[:], start=False, stop=True)
 
-        def top(n):
-            i = n // HEADS
-            minus_s[n] = work.tile([P, CHUNKS], F32, name="minus_s")
-            shift[n] = small.tile([P, 1], F32, name="shift")
-            nc.vector.tensor_scalar(
-                out=minus_s[n][:, 0 : width(i)],
-                in0=s_ps[n][:, 0 : width(i)],
-                scalar1=-SCALE,
-                scalar2=None,
-                op0=ALU.mult,
-                op1=ALU.min,
-                accum_out=shift[n][:],
-            )
+        def top(i, h0):
+            n, w = share(i), width(i)
+            top_s[i, h0] = small.tile([P, n], F32, name="top_s")
+            shift[i, h0] = small.tile([P, n], F32, name="shift")
+            nc.vector.tensor_reduce(out=top_s[i, h0][:], in_=s_ps[i, h0][:, :, 0:w], axis=AXIS.X, op=ALU.max)
+            nc.gpsimd.tensor_scalar(out=shift[i, h0][:], in0=top_s[i, h0][:], scalar1=-SCALE, scalar2=None, op0=ALU.mult)
 
-        def exponent(n):
-            i, h = divmod(n, HEADS)
-            nc.scalar.activation(
-                out=e_sb[h][:, 0 : width(i)],
-                in_=minus_s[n][:, 0 : width(i)],
-                func=ACT.Exp,
-                bias=shift[n][:],
-                scale=-1.0,
-                accum_out=sums[i][:, h : h + 1],
-            )
+        def exponent(i, h0):
+            n, w = share(i), width(i)
+            for b in range(n):
+                nc.scalar.activation(
+                    out=e_tile(i, h0)[:, b, 0:w],
+                    in_=s_ps[i, h0][:, b, 0:w],
+                    func=ACT.Exp,
+                    bias=shift[i, h0][:, b : b + 1],
+                    scale=SCALE,
+                    accum_out=sums[i][:, h0 + b : h0 + b + 1],
+                )
 
-        def turn_e(m):
-            a = m % PAIRS
-            e_ps[m] = turn_ps.tile([P, 2, 2, P], F32, tag="turn", name="e_ps")
+        def turn_e(i, h0):
+            n = share(i)
+            e_ps[i, h0] = turn_ps.tile([P, 2, 2, P], F32, tag="turn", name="e_ps")
             for b in range(2):
+                words = e_tile(i, h0 + b * n)[:].rearrange("p n j -> p (n j)").bitcast(F32)
                 for u in range(2):
-                    nc.tensor.transpose(e_ps[m][:, b, u, :], e_sb[2 * a + b][:].bitcast(F32)[:, u * P : (u + 1) * P], ident_f32[:])
+                    part = words[:, u * P : (u + 1) * P] if n == 1 else words[:, u : 2 * P : 2]
+                    nc.tensor.transpose(e_ps[i, h0][:, b, u, :], part, ident_f32[:])
 
-        def group_e(m):
-            e_grouped[m] = work.tile([P, 2, P, PACK], BF16, align_bytes=64, name="e_grouped")
-            nc.scalar.copy(out=e_grouped[m][:].bitcast(F32), in_=e_ps[m][:].rearrange("p b u r -> p b r u"))
+        def group_e(i, h0):
+            e_grouped[i, h0] = work.tile([P, 2, P, PACK], BF16, align_bytes=64, name="e_grouped")
+            nc.scalar.copy(out=e_grouped[i, h0][:].bitcast(F32), in_=e_ps[i, h0][:].rearrange("p b u r -> p b r u"))
 
-        def quantise_e(m):
-            e_codes[m] = work.tile([P, 2, P], U32, align_bytes=64, name="e_codes")
-            e_scales[m] = work.tile([P, 2, P], U8, align_bytes=64, name="e_scales")
+        def quantise_e(i, h0):
+            e_codes[i, h0] = work.tile([P, 2, P], U32, align_bytes=64, name="e_codes")
+            e_scales[i, h0] = work.tile([P, 2, P], U8, align_bytes=64, name="e_scales")
             nc.vector.quantize_mx(
-                out=e_codes[m][:].rearrange("p b r -> p (b r)").bitcast(FP8X4),
-                scales=e_scales[m][:].rearrange("p b r -> p (b r)"),
-                in_=e_grouped[m][:].rearrange("p b r t -> p (b r t)"),
+                out=e_codes[i, h0][:].rearrange("p b r -> p (b r)").bitcast(FP8X4),
+                scales=e_scales[i, h0][:].rearrange("p b r -> p (b r)"),
+                in_=e_grouped[i, h0][:].rearrange("p b r t -> p (b r t)"),
             )
 
-        def attend(x):
-            i_ps[x] = mx_ps.tile([P, PACK, D], F32, tag="mx", name="i_ps")
+        def attend(i, h0):
+            n = share(i)
+            i_ps[i, h0] = mx_ps.tile([P, PACK, D], F32, tag="mx", name="i_ps")
             for t in range(PACK):
-                h = PACK * (x % GROUPS) + t
-                m = 2 * x + t // 2
+                h = h0 + t
+                pair = (i, h // (2 * n) * (2 * n))
+                b = h // n % 2
                 nc.tensor.matmul_mx(
-                    out=i_ps[x][:, t, :],
-                    lhsT=e_codes[m][:, t % 2, :].bitcast(FP8X4),
-                    lhsT_scale=e_scales[m][:, t % 2, :],
-                    rhs=v_codes[:, h * D : (h + 1) * D].bitcast(FP8X4),
-                    rhs_scale=v_scales[:, h * D : (h + 1) * D],
+                    out=i_ps[i, h0][:, t, :],
+                    lhsT=e_codes[pair][:, b, :].bitcast(FP8X4),
+                    lhsT_scale=e_scales[pair][:, b, :],
+                    rhs=v_codes[n][:, h, :].bitcast(FP8X4),
+                    rhs_scale=v_scales[n][:, h // n, :],
                     start=True,
                     stop=True,
                 )
@@ -240,15 +302,14 @@ def tile_chunkedattention_pa_kernel(tc, q, k_means, v_means, intra, wo, bo, out)
             over_sum[i] = small.tile([P, HEADS], F32, name="over_sum")
             nc.vector.reciprocal(out=over_sum[i][:], in_=sums[i][:])
 
-        def fuse(x):
-            i, g = divmod(x, GROUPS)
-            if g == 0:
+        def fuse(i, h0):
+            if h0 == 0:
                 fused[i] = work.tile([P, HEADS, D], BF16, name="fused")
             for t in range(PACK):
-                h = PACK * g + t
+                h = h0 + t
                 nc.vector.scalar_tensor_tensor(
                     out=fused[i][:, h, :],
-                    in0=i_ps[x][:, t, :],
+                    in0=i_ps[i, h0][:, t, :],
                     scalar=over_sum[i][:, h : h + 1],
                     in1=intra_sb[i][:, h, :],
                     op0=ALU.mult,
@@ -274,12 +335,11 @@ def tile_chunkedattention_pa_kernel(tc, q, k_means, v_means, intra, wo, bo, out)
                 in_=f_grouped[i][:].rearrange("p g r t -> p (g r t)"),
             )
 
-        def project(y):
-            i, c = divmod(y, E // HALF)
-            o_ps[y] = mx_ps.tile([P, HALF], F32, tag="mx", name="o_ps")
+        def project(i, c):
+            o_ps[i, c] = mx_ps.tile([P, HALF], F32, tag="mx", name="o_ps")
             for g in range(GROUPS):
                 nc.tensor.matmul_mx(
-                    out=o_ps[y][:],
+                    out=o_ps[i, c][:],
                     lhsT=f_codes[i][:, g, :].bitcast(FP8X4),
                     lhsT_scale=f_scales[i][:, g, :],
                     rhs=wo_codes[:, g, c * HALF : (c + 1) * HALF].bitcast(FP8X4),
@@ -288,41 +348,62 @@ def tile_chunkedattention_pa_kernel(tc, q, k_means, v_means, intra, wo, bo, out)
                     stop=(g == GROUPS - 1),
                 )
 
-        def finish(y):
-            i, c = divmod(y, E // HALF)
+        def finish(i, c):
             cols = slice(c * HALF, (c + 1) * HALF)
             result = store.tile([P, HALF], F32)
-            nc.vector.tensor_tensor(out=result[:], in0=o_ps[y][:], in1=bias[:, cols], op=ALU.add)
+            nc.vector.tensor_tensor(out=result[:], in0=o_ps[i, c][:], in1=bias[:, cols], op=ALU.add)
             nc.sync.dma_start(out=out_rows[i * P : (i + 1) * P, cols], in_=result[:])
 
-        def run(step, tick, first, period, count):
-            x, rest = divmod(tick - first, period)
-            if rest == 0 and 0 <= x < count:
-                step(x)
+        steps = [top, finish, quantise_f, fuse, invert, quantise_e, group_v_shared, quantise_v_shared, spread_v, quantise_v, quantise_wo, zero_e, zero_v, group_f, group_e, exponent, keep_q, keep_k, group_wo, group_v, score, project, attend, turn_wo, turn_f, turn_e, turn_q, turn_k]
+        plan = {}
 
-        n_heads, n_pairs, n_fours, n_halves = TILES * HEADS, TILES * PAIRS, TILES * GROUPS, TILES * E // HALF
-        for tick in range(-9, n_heads + 42):
-            run(finish, tick, 44, 4, n_halves)
-            run(quantise_f, tick, 37, HEADS, TILES)
-            run(group_f, tick, 35, HEADS, TILES)
-            run(fuse, tick, 18, 4, n_fours)
-            run(invert, tick, 14, HEADS, TILES)
-            run(quantise_e, tick, 12, 2, n_pairs)
-            run(group_e, tick, 10, 2, n_pairs)
-            run(exponent, tick, 4, 1, n_heads)
-            run(top, tick, 2, 1, n_heads)
-            run(keep_q, tick, -3, HEADS, TILES)
-            run(keep_k, tick, -7, HEADS * PACK, PACK)
-            run(group_wo, tick, 8, 4, E // P)
-            if tick == 10:
-                quantise_v()
-            if tick == 38:
-                quantise_wo()
-            run(project, tick, 42, 4, n_halves)
-            run(attend, tick, 16, 4, n_fours)
-            run(turn_wo, tick, 6, 4, E // P)
-            run(turn_f, tick, 33, HEADS, TILES)
-            run(turn_e, tick, 8, 2, n_pairs)
-            run(turn_q, tick, -5, HEADS, TILES)
-            run(turn_k, tick, -9, HEADS * PACK, PACK)
-            run(score, tick, 0, 1, n_heads)
+        def due(tick, step, *what):
+            plan.setdefault(tick, []).append((steps.index(step), what))
+
+        for i in range(TILES):
+            n, first = share(i), HEADS * i
+            due(first - 5, turn_q, i)
+            due(first - 3, keep_q, i)
+            for h0 in range(0, HEADS, n):
+                due(first + h0, score, i, h0)
+                due(first + h0 + 1, top, i, h0)
+                due(first + h0 + 2, exponent, i, h0)
+            for h0 in range(0, HEADS, 2 * n):
+                turned = first + h0 + (10 if n == 4 else 8)
+                due(turned, turn_e, i, h0)
+                due(turned + 2, group_e, i, h0)
+                due(turned + 4, quantise_e, i, h0)
+            due(first + 14, invert, i)
+            for h0 in range(0, HEADS, PACK):
+                due(first + h0 + 16, attend, i, h0)
+                due(first + h0 + 16+2, fuse, i, h0)
+            due(first + 25, turn_f, i)
+            due(first + 25 + 2, group_f, i)
+            due(first + 25 + 4, quantise_f, i)
+            for c in range(E // HALF):
+                due(first + 4 * c + 34, project, i, c)
+                due(first + 4 * c + 34 + 2, finish, i, c)
+        for t in range(PACK):
+            due(HEADS * PACK * t - 9, turn_k, t)
+            due(HEADS * PACK * t - 7, keep_k, t)
+        for a in range(E // P):
+            due(2 * a + 0, turn_wo, a)
+            due(2 * a + 0 + 2, group_wo, a)
+        for g in range(GROUPS):
+            due(28 + 2 * g, quantise_wo, g)
+        for n, tick in ((4, 4), (2, 30)):
+            due(tick, group_v_shared, n)
+            due(tick + 2, quantise_v_shared, n)
+            due(tick + 4, spread_v, n)
+        for a in range(HEADS // 2):
+            due(44 + 4 * a, group_v, a)
+        due(60, quantise_v)
+        for r in range(e_sets[2]):
+            due(4 + 4 * r, zero_e, nc.gpsimd, 2, r)
+        due(22, zero_v, nc.gpsimd, 2)
+        for r in range(e_sets[1]):
+            due(26 + 4 * r, zero_e, nc.gpsimd, 1, r)
+
+        for tick in sorted(plan):
+            for number, what in sorted(plan[tick], key=lambda item: item[0]):
+                steps[number](*what)

@@ -40,6 +40,10 @@ def share(i):
     return 4 if width(i) <= 128 else 2 if width(i) <= 256 else 1
 
 
+FIRST = 4
+ORDER = list(range(TILES))
+
+
 def tile_chunkedattention_pa_kernel(tc, q, k_means, v_means, intra, wo, bo, out):
     nc = tc.nc
     q_rows = q.rearrange("b h c t d -> (b h) (c t) d")
@@ -53,6 +57,7 @@ def tile_chunkedattention_pa_kernel(tc, q, k_means, v_means, intra, wo, bo, out)
         keep = ctx.enter_context(tc.tile_pool(name="keep", bufs=1))
         work = ctx.enter_context(tc.tile_pool(name="work", bufs=4))
         small = ctx.enter_context(tc.tile_pool(name="small", bufs=6))
+        rows_in = ctx.enter_context(tc.tile_pool(name="rows_in", bufs=6))
         store = ctx.enter_context(tc.tile_pool(name="store", bufs=4))
         turn_ps = ctx.enter_context(tc.psum_pool(name="turn_ps", bufs=3))
         score_ps = ctx.enter_context(tc.psum_pool(name="score_ps", bufs=3))
@@ -61,48 +66,42 @@ def tile_chunkedattention_pa_kernel(tc, q, k_means, v_means, intra, wo, bo, out)
         k_sb = keep.tile([P, PACK, HEADS, D], BF16)
         wo_sb = keep.tile([P, E // P, E], BF16)
         bias = keep.tile([P, E], BF16)
-        q_sb = [keep.tile([P, HEADS, D], BF16, name="q_sb%d" % i) for i in range(TILES)]
-        intra_sb = [keep.tile([P, HEADS, D], BF16, name="intra_sb%d" % i) for i in range(TILES)]
+        q_sb, intra_sb = {}, {}
         v_sb = {
             1: keep.tile([P, PACK, HEADS, D], BF16, name="v_sb1"),
             2: keep.tile([P, HEADS // 2, PACK, D], BF16, name="v_sb2"),
             4: keep.tile([P, HEADS // 4, PACK, D], BF16, name="v_sb4"),
         }
 
-        def load_rows(tiles, rows, i):
-            nc.sync.dma_start(out=tiles[i][:], in_=rows[:, i * P : (i + 1) * P, :].rearrange("h p d -> p h d"))
+        wo_blocks = wo.rearrange("(a p) k -> a p k", p=P)
 
-        def load_v_shared(n):
+        def load_q(i):
+            q_sb[i] = rows_in.tile([P, HEADS, D], BF16, name="q_sb")
+            nc.sync.dma_start(out=q_sb[i][:], in_=q_rows[:, i * P : (i + 1) * P, :].rearrange("h p d -> p h d"))
+
+        def load_intra(i):
+            intra_sb[i] = rows_in.tile([P, HEADS, D], BF16, name="intra_sb")
+            nc.sync.dma_start(out=intra_sb[i][:], in_=intra_rows[:, i * P : (i + 1) * P, :].rearrange("h p d -> p h d"))
+
+        def load_k(t):
+            nc.sync.dma_start(out=k_sb[:, t], in_=k_blocks[t])
+
+        def load_wo(a):
+            nc.sync.dma_start(out=wo_sb[:, a, :], in_=wo_blocks[a])
+
+        def load_bias():
+            nc.sync.dma_start(out=bias[:], in_=bo.partition_broadcast(P))
+
+        def load_v(t):
+            nc.sync.dma_start(out=v_sb[1][:, t], in_=v_blocks[t // 2, t % 2])
+
+        def load_v_shared(n, s):
             rows = P // n
             heads = v_means.rearrange("b (a s) j d -> s (b a) j d", s=n)
-            for s in range(n):
-                nc.sync.dma_start(
-                    out=v_sb[n][s * rows : (s + 1) * rows],
-                    in_=heads[s, :, 0 : rows * PACK, :].rearrange("a (p t) d -> p a t d", t=PACK),
-                )
-
-        wo_blocks = wo.rearrange("(a p) k -> a p k", p=P)
-        nc.sync.dma_start(out=k_sb[:, 0], in_=k_blocks[0])
-        load_rows(q_sb, q_rows, 0)
-        load_rows(q_sb, q_rows, 1)
-        load_v_shared(4)
-        load_rows(intra_sb, intra_rows, 0)
-        for a in range(E // P):
-            nc.sync.dma_start(out=wo_sb[:, a, :], in_=wo_blocks[a])
-            if a == 3:
-                load_rows(q_sb, q_rows, 2)
-        load_rows(intra_sb, intra_rows, 1)
-        nc.sync.dma_start(out=bias[:], in_=bo.partition_broadcast(P))
-        load_v_shared(2)
-        for i in range(3, TILES):
-            load_rows(q_sb, q_rows, i)
-            load_rows(intra_sb, intra_rows, i - 1)
-            if i % PACK == 3 and i // PACK + 1 < PACK:
-                nc.sync.dma_start(out=k_sb[:, i // PACK + 1], in_=k_blocks[i // PACK + 1])
-            if i == 4:
-                for t in range(PACK):
-                    nc.sync.dma_start(out=v_sb[1][:, t], in_=v_blocks[t // 2, t % 2])
-        load_rows(intra_sb, intra_rows, TILES - 1)
+            nc.sync.dma_start(
+                out=v_sb[n][s * rows : (s + 1) * rows],
+                in_=heads[s, :, 0 : rows * PACK, :].rearrange("a (p t) d -> p a t d", t=PACK),
+            )
 
         ident = keep.tile([P, P], BF16)
         make_identity(nc, ident[:])
@@ -122,7 +121,7 @@ def tile_chunkedattention_pa_kernel(tc, q, k_means, v_means, intra, wo, bo, out)
         mask = keep.tile([P, TILE_CHUNKS], BF16)
         nc.vector.tensor_copy(out=mask[:], in_=mask_f32[:])
 
-        e_sets = {4: 4, 2: 4, 1: 8}
+        e_sets = {4: 8, 2: 4, 1: 8}
         e_sb, v_codes = {}, {}
         for n in (4, 2, 1):
             e_sb[n] = [keep.tile([P, n, CHUNKS // n], BF16, name="e_sb%d_%d" % (n, r)) for r in range(e_sets[n])]
@@ -134,9 +133,9 @@ def tile_chunkedattention_pa_kernel(tc, q, k_means, v_means, intra, wo, bo, out)
         def zero_v(engine, n):
             engine.memset(v_codes[n][:], 0)
 
-        for r in range(e_sets[4]):
-            zero_e(nc.vector, 4, r)
-        zero_v(nc.vector, 4)
+        for r in range(e_sets[FIRST]):
+            zero_e(nc.vector, FIRST, r)
+        zero_v(nc.vector, FIRST)
 
         warm = small.tile([P, 1], F32)
         nc.vector.memset(warm[:], 0.0)
@@ -273,8 +272,8 @@ def tile_chunkedattention_pa_kernel(tc, q, k_means, v_means, intra, wo, bo, out)
             nc.scalar.copy(out=e_grouped[i, h0][:].bitcast(F32), in_=e_ps[i, h0][:].rearrange("p b u r -> p b r u"))
 
         def quantise_e(i, h0):
-            e_codes[i, h0] = work.tile([P, 2, P], U32, align_bytes=64, name="e_codes")
-            e_scales[i, h0] = work.tile([P, 2, P], U8, align_bytes=64, name="e_scales")
+            e_codes[i, h0] = work.tile([P, 2, P], U32, align_bytes=64, name="e_codes", bufs=6)
+            e_scales[i, h0] = work.tile([P, 2, P], U8, align_bytes=64, name="e_scales", bufs=6)
             nc.vector.quantize_mx(
                 out=e_codes[i, h0][:].rearrange("p b r -> p (b r)").bitcast(FP8X4),
                 scales=e_scales[i, h0][:].rearrange("p b r -> p (b r)"),
@@ -354,55 +353,76 @@ def tile_chunkedattention_pa_kernel(tc, q, k_means, v_means, intra, wo, bo, out)
             nc.vector.tensor_tensor(out=result[:], in0=o_ps[i, c][:], in1=bias[:, cols], op=ALU.add)
             nc.sync.dma_start(out=out_rows[i * P : (i + 1) * P, cols], in_=result[:])
 
-        steps = [top, finish, quantise_f, fuse, invert, quantise_e, group_v_shared, quantise_v_shared, spread_v, quantise_v, quantise_wo, zero_e, zero_v, group_f, group_e, exponent, keep_q, keep_k, group_wo, group_v, score, project, attend, turn_wo, turn_f, turn_e, turn_q, turn_k]
+        steps = [load_k, load_q, load_v_shared, load_intra, load_wo, load_bias, load_v, top, finish, quantise_f, fuse, invert, quantise_e, group_v_shared, quantise_v_shared, spread_v, quantise_v, quantise_wo, zero_e, zero_v, group_f, group_e, exponent, keep_q, keep_k, group_wo, group_v, score, project, attend, turn_wo, turn_f, turn_e, turn_q, turn_k]
         plan = {}
+        early = [(load_k, 0), (load_q, 0), (load_q, 1), (load_v_shared, 4, 0), (load_v_shared, 4, 1), (load_v_shared, 4, 2), (load_v_shared, 4, 3), (load_intra, 0), (load_q, 2), (load_wo, 0), (load_wo, 1), (load_wo, 2), (load_wo, 3), (load_intra, 1), (load_wo, 4), (load_wo, 5), (load_wo, 6), (load_wo, 7), (load_q, 3), (load_bias,), (load_intra, 2), (load_v_shared, 2, 0), (load_v_shared, 2, 1), (load_k, 1), (load_q, 4), (load_intra, 3), (load_q, 5)]
+        for load in early:
+            load[0](*load[1:])
 
         def due(tick, step, *what):
             plan.setdefault(tick, []).append((steps.index(step), what))
 
-        for i in range(TILES):
-            n, first = share(i), HEADS * i
+        first = 0
+        ready_k = 0
+        for place, i in enumerate(ORDER):
+            n = share(i)
+            ticks = {4: 8, 2: 8, 1: 8}[n]
+            for step, lead in ((load_q, 30), (load_intra, 20)):
+                if (step, i) not in early:
+                    due(first - lead, step, i)
             due(first - 5, turn_q, i)
             due(first - 3, keep_q, i)
             for h0 in range(0, HEADS, n):
-                due(first + h0, score, i, h0)
-                due(first + h0 + 1, top, i, h0)
-                due(first + h0 + 2, exponent, i, h0)
+                at = first + h0 * ticks // HEADS
+                due(at, score, i, h0)
+                due(at + 1, top, i, h0)
+                due(at + 2, exponent, i, h0)
             for h0 in range(0, HEADS, 2 * n):
-                turned = first + h0 + (10 if n == 4 else 8)
+                turned = first + h0 * ticks // HEADS + {4: 10, 2: 8, 1: 8}[n]
                 due(turned, turn_e, i, h0)
                 due(turned + 2, group_e, i, h0)
                 due(turned + 4, quantise_e, i, h0)
             due(first + 14, invert, i)
-            for h0 in range(0, HEADS, PACK):
-                due(first + h0 + 16, attend, i, h0)
-                due(first + h0 + 16+2, fuse, i, h0)
-            due(first + 25, turn_f, i)
-            due(first + 25 + 2, group_f, i)
-            due(first + 25 + 4, quantise_f, i)
+            for x in range(HEADS // PACK):
+                at = first + 16 + x * ticks // 2
+                due(at, attend, i, x * PACK)
+                due(at + 2, fuse, i, x * PACK)
+            done = first + 16 + ticks // 2 + 2 + 0
+            due(done + 3, turn_f, i)
+            due(done + 3 + 2, group_f, i)
+            due(done + 3 + 4, quantise_f, i)
             for c in range(E // HALF):
-                due(first + 4 * c + 34, project, i, c)
-                due(first + 4 * c + 34 + 2, finish, i, c)
-        for t in range(PACK):
-            due(HEADS * PACK * t - 9, turn_k, t)
-            due(HEADS * PACK * t - 7, keep_k, t)
+                due(done + 12 + c * ticks // 2, project, i, c)
+                due(done + 12 + c * ticks // 2 + 2, finish, i, c)
+            new_k = -(-width(i) // P)
+            for t in range(ready_k, new_k):
+                if (load_k, t) not in early:
+                    due(first - 34, load_k, t)
+                due(first - 9 - 2 * (new_k - 1 - t), turn_k, t)
+                due(first - 9 - 2 * (new_k - 1 - t) + 2, keep_k, t)
+            ready_k = max(ready_k, new_k)
+            first += ticks
         for a in range(E // P):
             due(2 * a + 0, turn_wo, a)
             due(2 * a + 0 + 2, group_wo, a)
         for g in range(GROUPS):
             due(28 + 2 * g, quantise_wo, g)
         for n, tick in ((4, 4), (2, 30)):
+            for s in range(n):
+                if (load_v_shared, n, s) not in early:
+                    due(tick - 12, load_v_shared, n, s)
             due(tick, group_v_shared, n)
             due(tick + 2, quantise_v_shared, n)
             due(tick + 4, spread_v, n)
         for a in range(HEADS // 2):
+            due(44 - 24, load_v, a)
             due(44 + 4 * a, group_v, a)
-        due(60, quantise_v)
-        for r in range(e_sets[2]):
-            due(4 + 4 * r, zero_e, nc.gpsimd, 2, r)
-        due(22, zero_v, nc.gpsimd, 2)
-        for r in range(e_sets[1]):
-            due(26 + 4 * r, zero_e, nc.gpsimd, 1, r)
+        due(44 + 16, quantise_v)
+        for n, tick in ((2, 2), (1, 12)):
+            for r in range(e_sets[n]):
+                due(tick + 2 * r, zero_e, nc.gpsimd, n, r)
+            if n > 1:
+                due(tick, zero_v, nc.gpsimd, n)
 
         for tick in sorted(plan):
             for number, what in sorted(plan[tick], key=lambda item: item[0]):

@@ -40,7 +40,6 @@ def share(i):
     return 4 if width(i) <= 128 else 2 if width(i) <= 256 else 1
 
 
-FIRST = 4
 ORDER = list(range(TILES))
 
 
@@ -103,6 +102,10 @@ def tile_chunkedattention_pa_kernel(tc, q, k_means, v_means, intra, wo, bo, out)
                 in_=heads[s, :, 0 : rows * PACK, :].rearrange("a (p t) d -> p a t d", t=PACK),
             )
 
+        warm = small.tile([P, 1], F32)
+        nc.vector.memset(warm[:], 0.0)
+        nc.scalar.activation(out=warm[:], in_=warm[:], func=ACT.Exp)
+
         ident = keep.tile([P, P], BF16)
         make_identity(nc, ident[:])
         ident_f32 = keep.tile([P, P], F32)
@@ -119,7 +122,6 @@ def tile_chunkedattention_pa_kernel(tc, q, k_means, v_means, intra, wo, bo, out)
             channel_multiplier=1,
         )
         mask = keep.tile([P, TILE_CHUNKS], BF16)
-        nc.vector.tensor_copy(out=mask[:], in_=mask_f32[:])
 
         e_sets = {4: 8, 2: 4, 1: 8}
         e_sb, v_codes = {}, {}
@@ -127,19 +129,15 @@ def tile_chunkedattention_pa_kernel(tc, q, k_means, v_means, intra, wo, bo, out)
             e_sb[n] = [keep.tile([P, n, CHUNKS // n], BF16, name="e_sb%d_%d" % (n, r)) for r in range(e_sets[n])]
             v_codes[n] = keep.tile([P, HEADS, D], U32, align_bytes=64, name="v_codes%d" % n)
 
-        def zero_e(engine, n, r):
-            engine.memset(e_sb[n][r][:].rearrange("p n j -> p (n j)").bitcast(F32), 0.0)
+        for n, lowest, per_tile in ((4, 0, 2), (2, 4, 0), (1, 8, 0)):
+            for r in range(e_sets[n]):
+                never = e_sb[n][r][:].bitcast(F32)[:, :, width(lowest + (r // 2 if per_tile else 0)) // 2 :]
+                if never.shape[2]:
+                    nc.vector.memset(never, 0.0)
+            if n > 1:
+                nc.vector.memset(v_codes[n][:], 0)
 
-        def zero_v(engine, n):
-            engine.memset(v_codes[n][:], 0)
-
-        for r in range(e_sets[FIRST]):
-            zero_e(nc.vector, FIRST, r)
-        zero_v(nc.vector, FIRST)
-
-        warm = small.tile([P, 1], F32)
-        nc.vector.memset(warm[:], 0.0)
-        nc.scalar.activation(out=warm[:], in_=warm[:], func=ACT.Exp)
+        nc.vector.tensor_copy(out=mask[:], in_=mask_f32[:])
 
         k_t = keep.tile([P, HEADS, CHUNKS], BF16)
 
@@ -153,6 +151,9 @@ def tile_chunkedattention_pa_kernel(tc, q, k_means, v_means, intra, wo, bo, out)
         def keep_k(t):
             nc.scalar.copy(out=k_t[:, :, t * P : (t + 1) * P], in_=k_ps[t][:])
 
+        def copy_gpsimd(out, in_):
+            nc.gpsimd.tensor_scalar(out=out, in0=in_, scalar1=1.0, scalar2=0.0, op0=ALU.mult, op1=ALU.add)
+
         v_grouped = {1: keep.tile([P, HEADS, D, PACK], BF16, align_bytes=64, name="v_grouped1")}
         v_scales = {1: keep.tile([P, HEADS, D], U8, align_bytes=64, name="v_scales1")}
         v_dense = {}
@@ -161,8 +162,8 @@ def tile_chunkedattention_pa_kernel(tc, q, k_means, v_means, intra, wo, bo, out)
             v_scales[n] = keep.tile([P, HEADS // n, D], U8, align_bytes=64, name="v_scales%d" % n)
             v_dense[n] = keep.tile([P, HEADS // n, D], U32, align_bytes=64, name="v_dense%d" % n)
 
-        def group_v_shared(n):
-            nc.vector.tensor_copy(out=v_grouped[n][:], in_=v_sb[n][:].rearrange("p a t d -> p a d t"))
+        def group_v_shared(n, a):
+            (nc.vector.tensor_copy if n == 4 else copy_gpsimd)(out=v_grouped[n][:, a], in_=v_sb[n][:, a].rearrange("p t d -> p d t"))
 
         def quantise_v_shared(n):
             nc.vector.quantize_mx(
@@ -178,9 +179,8 @@ def tile_chunkedattention_pa_kernel(tc, q, k_means, v_means, intra, wo, bo, out)
                 part = slice(s * rows, (s + 1) * rows)
                 nc.vector.tensor_copy(out=heads[part, :, s, :].bitcast(I32), in_=v_dense[n][part].bitcast(I32))
 
-        def group_v(a):
-            heads = slice(2 * a, 2 * a + 2)
-            nc.scalar.copy(out=v_grouped[1][:, heads], in_=v_sb[1][:, :, heads, :].rearrange("p t h d -> p h d t"))
+        def group_v(h):
+            copy_gpsimd(v_grouped[1][:, h], v_sb[1][:, :, h, :].rearrange("p t d -> p d t"))
 
         def quantise_v():
             nc.vector.quantize_mx(
@@ -213,7 +213,7 @@ def tile_chunkedattention_pa_kernel(tc, q, k_means, v_means, intra, wo, bo, out)
                 in_=wo_grouped[:, g].rearrange("p o t -> p (o t)"),
             )
 
-        q_ps, q_t, s_ps, top_s, shift, sums = {}, {}, {}, {}, {}, {}
+        minus_s, q_ps, q_t, s_ps, top_s, shift, sums = {}, {}, {}, {}, {}, {}, {}
         e_ps, e_grouped, e_codes, e_scales, i_ps, over_sum, fused = {}, {}, {}, {}, {}, {}, {}
         f_ps, f_grouped, f_codes, f_scales, o_ps = {}, {}, {}, {}, {}
 
@@ -243,6 +243,18 @@ def tile_chunkedattention_pa_kernel(tc, q, k_means, v_means, intra, wo, bo, out)
             n, w = share(i), width(i)
             top_s[i, h0] = small.tile([P, n], F32, name="top_s")
             shift[i, h0] = small.tile([P, n], F32, name="shift")
+            if n == 1:
+                minus_s[i, h0] = work.tile([P, CHUNKS], F32, name="minus_s")
+                nc.vector.tensor_scalar(
+                    out=minus_s[i, h0][:, 0:w],
+                    in0=s_ps[i, h0][:, 0, 0:w],
+                    scalar1=-SCALE,
+                    scalar2=None,
+                    op0=ALU.mult,
+                    op1=ALU.min,
+                    accum_out=shift[i, h0][:],
+                )
+                return
             nc.vector.tensor_reduce(out=top_s[i, h0][:], in_=s_ps[i, h0][:, :, 0:w], axis=AXIS.X, op=ALU.max)
             nc.gpsimd.tensor_scalar(out=shift[i, h0][:], in0=top_s[i, h0][:], scalar1=-SCALE, scalar2=None, op0=ALU.mult)
 
@@ -251,10 +263,10 @@ def tile_chunkedattention_pa_kernel(tc, q, k_means, v_means, intra, wo, bo, out)
             for b in range(n):
                 nc.scalar.activation(
                     out=e_tile(i, h0)[:, b, 0:w],
-                    in_=s_ps[i, h0][:, b, 0:w],
+                    in_=minus_s[i, h0][:, 0:w] if n == 1 else s_ps[i, h0][:, b, 0:w],
                     func=ACT.Exp,
                     bias=shift[i, h0][:, b : b + 1],
-                    scale=SCALE,
+                    scale=-1.0 if n == 1 else SCALE,
                     accum_out=sums[i][:, h0 + b : h0 + b + 1],
                 )
 
@@ -301,10 +313,10 @@ def tile_chunkedattention_pa_kernel(tc, q, k_means, v_means, intra, wo, bo, out)
             over_sum[i] = small.tile([P, HEADS], F32, name="over_sum")
             nc.vector.reciprocal(out=over_sum[i][:], in_=sums[i][:])
 
-        def fuse(i, h0):
-            if h0 == 0:
+        def fuse(i, h0, heads):
+            if h0 + heads[0] == 0:
                 fused[i] = work.tile([P, HEADS, D], BF16, name="fused")
-            for t in range(PACK):
+            for t in heads:
                 h = h0 + t
                 nc.vector.scalar_tensor_tensor(
                     out=fused[i][:, h, :],
@@ -349,13 +361,21 @@ def tile_chunkedattention_pa_kernel(tc, q, k_means, v_means, intra, wo, bo, out)
 
         def finish(i, c):
             cols = slice(c * HALF, (c + 1) * HALF)
-            result = store.tile([P, HALF], F32)
+            result = store.tile([P, HALF], F32, name="result")
             nc.vector.tensor_tensor(out=result[:], in0=o_ps[i, c][:], in1=bias[:, cols], op=ALU.add)
             nc.sync.dma_start(out=out_rows[i * P : (i + 1) * P, cols], in_=result[:])
 
-        steps = [load_k, load_q, load_v_shared, load_intra, load_wo, load_bias, load_v, top, finish, quantise_f, fuse, invert, quantise_e, group_v_shared, quantise_v_shared, spread_v, quantise_v, quantise_wo, zero_e, zero_v, group_f, group_e, exponent, keep_q, keep_k, group_wo, group_v, score, project, attend, turn_wo, turn_f, turn_e, turn_q, turn_k]
+        def finish_aside(i, c):
+            cols = slice(c * HALF, (c + 1) * HALF)
+            product = store.tile([P, HALF], F32, name="product", bufs=2)
+            nc.scalar.copy(out=product[:], in_=o_ps[i, c][:])
+            result = store.tile([P, HALF], F32, name="result")
+            nc.gpsimd.tensor_tensor(out=result[:], in0=product[:], in1=bias[:, cols], op=ALU.add)
+            nc.sync.dma_start(out=out_rows[i * P : (i + 1) * P, cols], in_=result[:])
+
+        steps = [load_k, load_q, load_v_shared, load_intra, load_wo, load_bias, load_v, top, finish, quantise_f, fuse, invert, quantise_e, quantise_v_shared, spread_v, quantise_v, quantise_wo, finish_aside, group_f, group_e, exponent, keep_q, keep_k, group_wo, group_v, group_v_shared, score, project, attend, turn_wo, turn_f, turn_e, turn_q, turn_k]
         plan = {}
-        early = [(load_k, 0), (load_q, 0), (load_q, 1), (load_v_shared, 4, 0), (load_v_shared, 4, 1), (load_v_shared, 4, 2), (load_v_shared, 4, 3), (load_intra, 0), (load_q, 2), (load_wo, 0), (load_wo, 1), (load_wo, 2), (load_wo, 3), (load_intra, 1), (load_wo, 4), (load_wo, 5), (load_wo, 6), (load_wo, 7), (load_q, 3), (load_bias,), (load_intra, 2), (load_v_shared, 2, 0), (load_v_shared, 2, 1), (load_k, 1), (load_q, 4), (load_intra, 3), (load_q, 5)]
+        early = [(load_k, 0), (load_q, 0), (load_v_shared, 4, 0), (load_v_shared, 4, 1), (load_v_shared, 4, 2), (load_v_shared, 4, 3), (load_q, 1), (load_intra, 0), (load_wo, 0), (load_wo, 1), (load_q, 2), (load_wo, 2), (load_wo, 3), (load_intra, 1), (load_wo, 4), (load_wo, 5), (load_q, 3), (load_wo, 6), (load_wo, 7), (load_k, 1), (load_intra, 2), (load_v_shared, 2, 0), (load_v_shared, 2, 1), (load_q, 4), (load_bias,), (load_intra, 3), (load_q, 5)]
         for load in early:
             load[0](*load[1:])
 
@@ -376,7 +396,7 @@ def tile_chunkedattention_pa_kernel(tc, q, k_means, v_means, intra, wo, bo, out)
                 at = first + h0 * ticks // HEADS
                 due(at, score, i, h0)
                 due(at + 1, top, i, h0)
-                due(at + 2, exponent, i, h0)
+                due(at + (3 if n == 1 else 2), exponent, i, h0)
             for h0 in range(0, HEADS, 2 * n):
                 turned = first + h0 * ticks // HEADS + {4: 10, 2: 8, 1: 8}[n]
                 due(turned, turn_e, i, h0)
@@ -386,14 +406,15 @@ def tile_chunkedattention_pa_kernel(tc, q, k_means, v_means, intra, wo, bo, out)
             for x in range(HEADS // PACK):
                 at = first + 16 + x * ticks // 2
                 due(at, attend, i, x * PACK)
-                due(at + 2, fuse, i, x * PACK)
+                due(at + 2, fuse, i, x * PACK, (0, 1))
+                due(at + 2, fuse, i, x * PACK, (2, 3))
             done = first + 16 + ticks // 2 + 2 + 0
             due(done + 3, turn_f, i)
             due(done + 3 + 2, group_f, i)
             due(done + 3 + 4, quantise_f, i)
             for c in range(E // HALF):
                 due(done + 12 + c * ticks // 2, project, i, c)
-                due(done + 12 + c * ticks // 2 + 2, finish, i, c)
+                due(done + 12 + c * ticks // 2 + 2, finish_aside if False else finish, i, c)
             new_k = -(-width(i) // P)
             for t in range(ready_k, new_k):
                 if (load_k, t) not in early:
@@ -403,26 +424,23 @@ def tile_chunkedattention_pa_kernel(tc, q, k_means, v_means, intra, wo, bo, out)
             ready_k = max(ready_k, new_k)
             first += ticks
         for a in range(E // P):
-            due(2 * a + 0, turn_wo, a)
-            due(2 * a + 0 + 2, group_wo, a)
+            due(2 * a + 9, turn_wo, a)
+            due(2 * a + 9 + 2, group_wo, a)
         for g in range(GROUPS):
             due(28 + 2 * g, quantise_wo, g)
-        for n, tick in ((4, 4), (2, 30)):
+        for n, tick in ((4, 4), (2, 20)):
             for s in range(n):
                 if (load_v_shared, n, s) not in early:
                     due(tick - 12, load_v_shared, n, s)
-            due(tick, group_v_shared, n)
-            due(tick + 2, quantise_v_shared, n)
-            due(tick + 4, spread_v, n)
+            for a in range(HEADS // n):
+                due(tick + 2 * a, group_v_shared, n, a)
+            due(tick + (4 if n == 4 else 10), quantise_v_shared, n)
+            due(tick + (4 if n == 4 else 10) + 2, spread_v, n)
         for a in range(HEADS // 2):
-            due(44 - 24, load_v, a)
-            due(44 + 4 * a, group_v, a)
-        due(44 + 16, quantise_v)
-        for n, tick in ((2, 2), (1, 12)):
-            for r in range(e_sets[n]):
-                due(tick + 2 * r, zero_e, nc.gpsimd, n, r)
-            if n > 1:
-                due(tick, zero_v, nc.gpsimd, n)
+            due(40 - 40, load_v, a)
+        for h in range(HEADS):
+            due(40 + 2 * h, group_v, h)
+        due(40 + 24, quantise_v)
 
         for tick in sorted(plan):
             for number, what in sorted(plan[tick], key=lambda item: item[0]):

@@ -48,7 +48,7 @@ def tile_chunkedattention_pa_kernel(tc, q, k_means, v_means, intra, wo, bo, out)
     q_rows = q.rearrange("b h c t d -> (b h) (c t) d")
     intra_rows = intra.rearrange("b h c t d -> (b h) (c t) d")
     k_blocks = k_means.rearrange("b h (t p) d -> t p (b h) d", p=P)
-    v_blocks = v_means.rearrange("b h (u p e) d -> u e p (b h) d", p=P, e=2)
+    v_blocks = v_means.rearrange("b h (u p e) d -> u p (b h) e d", p=P, e=2)
     out_rows = out.rearrange("b s o -> (b s) o")
 
     with ExitStack() as ctx:
@@ -67,7 +67,7 @@ def tile_chunkedattention_pa_kernel(tc, q, k_means, v_means, intra, wo, bo, out)
         bias = keep.tile([P, E], BF16)
         q_sb, intra_sb = {}, {}
         v_sb = {
-            1: keep.tile([P, PACK, HEADS, D], BF16, name="v_sb1"),
+            1: keep.tile([P, 2, HEADS, 2, D], BF16, name="v_sb1"),
             2: keep.tile([P, HEADS // 2, PACK, D], BF16, name="v_sb2"),
             4: keep.tile([P, HEADS // 4, PACK, D], BF16, name="v_sb4"),
         }
@@ -86,13 +86,13 @@ def tile_chunkedattention_pa_kernel(tc, q, k_means, v_means, intra, wo, bo, out)
             nc.sync.dma_start(out=k_sb[:, t], in_=k_blocks[t])
 
         def load_wo(a):
-            nc.sync.dma_start(out=wo_sb[:, a, :], in_=wo_blocks[a])
+            nc.sync.dma_start(out=wo_sb[:, a : a + 2, :], in_=wo_blocks[a : a + 2].rearrange("a p k -> p a k"))
 
         def load_bias():
             nc.sync.dma_start(out=bias[:], in_=bo.partition_broadcast(P))
 
-        def load_v(t):
-            nc.sync.dma_start(out=v_sb[1][:, t], in_=v_blocks[t // 2, t % 2])
+        def load_v(u):
+            nc.sync.dma_start(out=v_sb[1][:, u], in_=v_blocks[u])
 
         def load_v_shared(n, s):
             rows = P // n
@@ -180,7 +180,7 @@ def tile_chunkedattention_pa_kernel(tc, q, k_means, v_means, intra, wo, bo, out)
                 nc.vector.tensor_copy(out=heads[part, :, s, :].bitcast(I32), in_=v_dense[n][part].bitcast(I32))
 
         def group_v(h):
-            copy_gpsimd(v_grouped[1][:, h], v_sb[1][:, :, h, :].rearrange("p t d -> p d t"))
+            copy_gpsimd(out=v_grouped[1][:, h].rearrange("p d (u e) -> p d u e", e=2), in_=v_sb[1][:, :, h].rearrange("p u e d -> p d u e"))
 
         def quantise_v():
             nc.vector.quantize_mx(
@@ -213,7 +213,7 @@ def tile_chunkedattention_pa_kernel(tc, q, k_means, v_means, intra, wo, bo, out)
                 in_=wo_grouped[:, g].rearrange("p o t -> p (o t)"),
             )
 
-        minus_s, q_ps, q_t, s_ps, top_s, shift, sums = {}, {}, {}, {}, {}, {}, {}
+        q_ps, q_t, s_ps, top_s, shift, sums = {}, {}, {}, {}, {}, {}
         e_ps, e_grouped, e_codes, e_scales, i_ps, over_sum, fused = {}, {}, {}, {}, {}, {}, {}
         f_ps, f_grouped, f_codes, f_scales, o_ps = {}, {}, {}, {}, {}
 
@@ -243,18 +243,6 @@ def tile_chunkedattention_pa_kernel(tc, q, k_means, v_means, intra, wo, bo, out)
             n, w = share(i), width(i)
             top_s[i, h0] = small.tile([P, n], F32, name="top_s")
             shift[i, h0] = small.tile([P, n], F32, name="shift")
-            if n == 1:
-                minus_s[i, h0] = work.tile([P, CHUNKS], F32, name="minus_s")
-                nc.vector.tensor_scalar(
-                    out=minus_s[i, h0][:, 0:w],
-                    in0=s_ps[i, h0][:, 0, 0:w],
-                    scalar1=-SCALE,
-                    scalar2=None,
-                    op0=ALU.mult,
-                    op1=ALU.min,
-                    accum_out=shift[i, h0][:],
-                )
-                return
             nc.vector.tensor_reduce(out=top_s[i, h0][:], in_=s_ps[i, h0][:, :, 0:w], axis=AXIS.X, op=ALU.max)
             nc.gpsimd.tensor_scalar(out=shift[i, h0][:], in0=top_s[i, h0][:], scalar1=-SCALE, scalar2=None, op0=ALU.mult)
 
@@ -263,12 +251,17 @@ def tile_chunkedattention_pa_kernel(tc, q, k_means, v_means, intra, wo, bo, out)
             for b in range(n):
                 nc.scalar.activation(
                     out=e_tile(i, h0)[:, b, 0:w],
-                    in_=minus_s[i, h0][:, 0:w] if n == 1 else s_ps[i, h0][:, b, 0:w],
+                    in_=s_ps[i, h0][:, b, 0:w],
                     func=ACT.Exp,
                     bias=shift[i, h0][:, b : b + 1],
-                    scale=-1.0 if n == 1 else SCALE,
+                    scale=SCALE,
                     accum_out=sums[i][:, h0 + b : h0 + b + 1],
                 )
+
+        def run_of(i, h):
+            units = 4 if share(i) == 1 else 2
+            heads = units * share(i)
+            return h // heads * heads, units
 
         def turn_e(i, h0):
             n = share(i)
@@ -280,12 +273,21 @@ def tile_chunkedattention_pa_kernel(tc, q, k_means, v_means, intra, wo, bo, out)
                     nc.tensor.transpose(e_ps[i, h0][:, b, u, :], part, ident_f32[:])
 
         def group_e(i, h0):
-            e_grouped[i, h0] = work.tile([P, 2, P, PACK], BF16, align_bytes=64, name="e_grouped")
-            nc.scalar.copy(out=e_grouped[i, h0][:].bitcast(F32), in_=e_ps[i, h0][:].rearrange("p b u r -> p b r u"))
+            first, units = run_of(i, h0)
+            if h0 == first:
+                e_grouped[i, h0] = work.tile([P, units, P, PACK], BF16, align_bytes=64, name="e_grouped%d" % units)
+            place = (h0 - first) // share(i)
+            nc.scalar.copy(
+                out=e_grouped[i, first][:, place : place + 2].bitcast(F32), in_=e_ps[i, h0][:].rearrange("p b u r -> p b r u")
+            )
 
         def quantise_e(i, h0):
-            e_codes[i, h0] = work.tile([P, 2, P], U32, align_bytes=64, name="e_codes", bufs=6)
-            e_scales[i, h0] = work.tile([P, 2, P], U8, align_bytes=64, name="e_scales", bufs=6)
+            first, units = run_of(i, h0)
+            if h0 + 2 * share(i) < first + units * share(i):
+                return
+            h0 = first
+            e_codes[i, h0] = work.tile([P, units, P], U32, align_bytes=64, name="e_codes%d" % units)
+            e_scales[i, h0] = work.tile([P, units, P], U8, align_bytes=64, name="e_scales%d" % units)
             nc.vector.quantize_mx(
                 out=e_codes[i, h0][:].rearrange("p b r -> p (b r)").bitcast(FP8X4),
                 scales=e_scales[i, h0][:].rearrange("p b r -> p (b r)"),
@@ -297,8 +299,9 @@ def tile_chunkedattention_pa_kernel(tc, q, k_means, v_means, intra, wo, bo, out)
             i_ps[i, h0] = mx_ps.tile([P, PACK, D], F32, tag="mx", name="i_ps")
             for t in range(PACK):
                 h = h0 + t
-                pair = (i, h // (2 * n) * (2 * n))
-                b = h // n % 2
+                first, units = run_of(i, h)
+                pair = (i, first)
+                b = (h - first) // n
                 nc.tensor.matmul_mx(
                     out=i_ps[i, h0][:, t, :],
                     lhsT=e_codes[pair][:, b, :].bitcast(FP8X4),
@@ -375,7 +378,7 @@ def tile_chunkedattention_pa_kernel(tc, q, k_means, v_means, intra, wo, bo, out)
 
         steps = [load_k, load_q, load_v_shared, load_intra, load_wo, load_bias, load_v, top, finish, quantise_f, fuse, invert, quantise_e, quantise_v_shared, spread_v, quantise_v, quantise_wo, finish_aside, group_f, group_e, exponent, keep_q, keep_k, group_wo, group_v, group_v_shared, score, project, attend, turn_wo, turn_f, turn_e, turn_q, turn_k]
         plan = {}
-        early = [(load_k, 0), (load_q, 0), (load_v_shared, 4, 0), (load_v_shared, 4, 1), (load_v_shared, 4, 2), (load_v_shared, 4, 3), (load_q, 1), (load_intra, 0), (load_wo, 0), (load_wo, 1), (load_q, 2), (load_wo, 2), (load_wo, 3), (load_intra, 1), (load_wo, 4), (load_wo, 5), (load_q, 3), (load_wo, 6), (load_wo, 7), (load_k, 1), (load_intra, 2), (load_v_shared, 2, 0), (load_v_shared, 2, 1), (load_q, 4), (load_bias,), (load_intra, 3), (load_q, 5)]
+        early = [(load_k, 0), (load_q, 0), (load_v_shared, 4, 0), (load_v_shared, 4, 1), (load_v_shared, 4, 2), (load_v_shared, 4, 3), (load_q, 1), (load_intra, 0), (load_wo, 0), (load_q, 2), (load_wo, 2), (load_intra, 1), (load_wo, 4), (load_q, 3), (load_wo, 6), (load_intra, 2), (load_k, 1), (load_q, 4), (load_v_shared, 2, 0), (load_v_shared, 2, 1), (load_bias,), (load_intra, 3), (load_q, 5)]
         for load in early:
             load[0](*load[1:])
 
@@ -396,7 +399,7 @@ def tile_chunkedattention_pa_kernel(tc, q, k_means, v_means, intra, wo, bo, out)
                 at = first + h0 * ticks // HEADS
                 due(at, score, i, h0)
                 due(at + 1, top, i, h0)
-                due(at + (3 if n == 1 else 2), exponent, i, h0)
+                due(at + 2, exponent, i, h0)
             for h0 in range(0, HEADS, 2 * n):
                 turned = first + h0 * ticks // HEADS + {4: 10, 2: 8, 1: 8}[n]
                 due(turned, turn_e, i, h0)
@@ -428,16 +431,17 @@ def tile_chunkedattention_pa_kernel(tc, q, k_means, v_means, intra, wo, bo, out)
             due(2 * a + 9 + 2, group_wo, a)
         for g in range(GROUPS):
             due(28 + 2 * g, quantise_wo, g)
-        for n, tick in ((4, 4), (2, 20)):
+        for n, tick in ((4, 4), (2, 28)):
             for s in range(n):
                 if (load_v_shared, n, s) not in early:
                     due(tick - 12, load_v_shared, n, s)
             for a in range(HEADS // n):
                 due(tick + 2 * a, group_v_shared, n, a)
-            due(tick + (4 if n == 4 else 10), quantise_v_shared, n)
-            due(tick + (4 if n == 4 else 10) + 2, spread_v, n)
-        for a in range(HEADS // 2):
-            due(40 - 40, load_v, a)
+            due(tick + (4 if n == 4 else 14), quantise_v_shared, n)
+            due(tick + (4 if n == 4 else 14) + 2, spread_v, n)
+        for u in range(2):
+            if (load_v, u) not in early:
+                due(40 - 40, load_v, u)
         for h in range(HEADS):
             due(40 + 2 * h, group_v, h)
         due(40 + 24, quantise_v)

@@ -163,7 +163,7 @@ def tile_chunkedattention_pa_kernel(tc, q, k_means, v_means, intra, wo, bo, out)
             v_dense[n] = keep.tile([P, HEADS // n, D], U32, align_bytes=64, name="v_dense%d" % n)
 
         def group_v_shared(n, a):
-            (nc.vector.tensor_copy if n == 4 else copy_gpsimd)(out=v_grouped[n][:, a], in_=v_sb[n][:, a].rearrange("p t d -> p d t"))
+            (nc.vector.tensor_copy if n == 4 else nc.scalar.copy)(out=v_grouped[n][:, a], in_=v_sb[n][:, a].rearrange("p t d -> p d t"))
 
         def quantise_v_shared(n):
             nc.vector.quantize_mx(
@@ -180,7 +180,7 @@ def tile_chunkedattention_pa_kernel(tc, q, k_means, v_means, intra, wo, bo, out)
                 nc.vector.tensor_copy(out=heads[part, :, s, :].bitcast(I32), in_=v_dense[n][part].bitcast(I32))
 
         def group_v(h):
-            copy_gpsimd(out=v_grouped[1][:, h].rearrange("p d (u e) -> p d u e", e=2), in_=v_sb[1][:, :, h].rearrange("p u e d -> p d u e"))
+            nc.scalar.copy(out=v_grouped[1][:, h].rearrange("p d (u e) -> p d u e", e=2), in_=v_sb[1][:, :, h].rearrange("p u e d -> p d u e"))
 
         def quantise_v():
             nc.vector.quantize_mx(
@@ -213,7 +213,7 @@ def tile_chunkedattention_pa_kernel(tc, q, k_means, v_means, intra, wo, bo, out)
                 in_=wo_grouped[:, g].rearrange("p o t -> p (o t)"),
             )
 
-        q_ps, q_t, s_ps, top_s, shift, sums = {}, {}, {}, {}, {}, {}
+        minus_s, q_ps, q_t, s_ps, top_s, shift, sums = {}, {}, {}, {}, {}, {}, {}
         e_ps, e_grouped, e_codes, e_scales, i_ps, over_sum, fused = {}, {}, {}, {}, {}, {}, {}
         f_ps, f_grouped, f_codes, f_scales, o_ps = {}, {}, {}, {}, {}
 
@@ -243,6 +243,18 @@ def tile_chunkedattention_pa_kernel(tc, q, k_means, v_means, intra, wo, bo, out)
             n, w = share(i), width(i)
             top_s[i, h0] = small.tile([P, n], F32, name="top_s")
             shift[i, h0] = small.tile([P, n], F32, name="shift")
+            if n == 1:
+                minus_s[i, h0] = work.tile([P, CHUNKS], F32, name="minus_s")
+                nc.vector.tensor_scalar(
+                    out=minus_s[i, h0][:, 0:w],
+                    in0=s_ps[i, h0][:, 0, 0:w],
+                    scalar1=-SCALE,
+                    scalar2=None,
+                    op0=ALU.mult,
+                    op1=ALU.min,
+                    accum_out=shift[i, h0][:],
+                )
+                return
             nc.vector.tensor_reduce(out=top_s[i, h0][:], in_=s_ps[i, h0][:, :, 0:w], axis=AXIS.X, op=ALU.max)
             nc.gpsimd.tensor_scalar(out=shift[i, h0][:], in0=top_s[i, h0][:], scalar1=-SCALE, scalar2=None, op0=ALU.mult)
 
@@ -251,10 +263,10 @@ def tile_chunkedattention_pa_kernel(tc, q, k_means, v_means, intra, wo, bo, out)
             for b in range(n):
                 nc.scalar.activation(
                     out=e_tile(i, h0)[:, b, 0:w],
-                    in_=s_ps[i, h0][:, b, 0:w],
+                    in_=minus_s[i, h0][:, 0:w] if n == 1 else s_ps[i, h0][:, b, 0:w],
                     func=ACT.Exp,
                     bias=shift[i, h0][:, b : b + 1],
-                    scale=SCALE,
+                    scale=-1.0 if n == 1 else SCALE,
                     accum_out=sums[i][:, h0 + b : h0 + b + 1],
                 )
 
@@ -275,7 +287,7 @@ def tile_chunkedattention_pa_kernel(tc, q, k_means, v_means, intra, wo, bo, out)
         def group_e(i, h0):
             first, units = run_of(i, h0)
             if h0 == first:
-                e_grouped[i, h0] = work.tile([P, units, P, PACK], BF16, align_bytes=64, name="e_grouped%d" % units)
+                e_grouped[i, h0] = work.tile([P, units, P, PACK], BF16, align_bytes=64, name="e_grouped%d" % units, bufs=3)
             place = (h0 - first) // share(i)
             nc.scalar.copy(
                 out=e_grouped[i, first][:, place : place + 2].bitcast(F32), in_=e_ps[i, h0][:].rearrange("p b u r -> p b r u")
@@ -376,7 +388,7 @@ def tile_chunkedattention_pa_kernel(tc, q, k_means, v_means, intra, wo, bo, out)
             nc.gpsimd.tensor_tensor(out=result[:], in0=product[:], in1=bias[:, cols], op=ALU.add)
             nc.sync.dma_start(out=out_rows[i * P : (i + 1) * P, cols], in_=result[:])
 
-        steps = [load_k, load_q, load_v_shared, load_intra, load_wo, load_bias, load_v, top, finish, quantise_f, fuse, invert, quantise_e, quantise_v_shared, spread_v, quantise_v, quantise_wo, finish_aside, group_f, group_e, exponent, keep_q, keep_k, group_wo, group_v, group_v_shared, score, project, attend, turn_wo, turn_f, turn_e, turn_q, turn_k]
+        steps = [load_k, load_q, load_v_shared, load_intra, load_wo, load_bias, load_v, top, finish, quantise_f, fuse, invert, quantise_e, quantise_v_shared, spread_v, quantise_v, quantise_wo, group_f, group_e, exponent, keep_q, keep_k, group_wo, finish_aside, group_v, group_v_shared, score, project, attend, turn_wo, turn_f, turn_e, turn_q, turn_k]
         plan = {}
         early = [(load_k, 0), (load_q, 0), (load_v_shared, 4, 0), (load_v_shared, 4, 1), (load_v_shared, 4, 2), (load_v_shared, 4, 3), (load_q, 1), (load_intra, 0), (load_wo, 0), (load_q, 2), (load_wo, 2), (load_intra, 1), (load_wo, 4), (load_q, 3), (load_wo, 6), (load_intra, 2), (load_k, 1), (load_q, 4), (load_v_shared, 2, 0), (load_v_shared, 2, 1), (load_bias,), (load_intra, 3), (load_q, 5)]
         for load in early:
@@ -399,7 +411,7 @@ def tile_chunkedattention_pa_kernel(tc, q, k_means, v_means, intra, wo, bo, out)
                 at = first + h0 * ticks // HEADS
                 due(at, score, i, h0)
                 due(at + 1, top, i, h0)
-                due(at + 2, exponent, i, h0)
+                due(at + (3 if n == 1 else 2), exponent, i, h0)
             for h0 in range(0, HEADS, 2 * n):
                 turned = first + h0 * ticks // HEADS + {4: 10, 2: 8, 1: 8}[n]
                 due(turned, turn_e, i, h0)
@@ -417,7 +429,10 @@ def tile_chunkedattention_pa_kernel(tc, q, k_means, v_means, intra, wo, bo, out)
             due(done + 3 + 4, quantise_f, i)
             for c in range(E // HALF):
                 due(done + 12 + c * ticks // 2, project, i, c)
-                due(done + 12 + c * ticks // 2 + 2, finish_aside if False else finish, i, c)
+                if c == 1 and 3 < i < 12:
+                    due(done + 12 + c * ticks // 2 + 1, finish_aside, i, c)
+                else:
+                    due(done + 12 + c * ticks // 2 + 2, finish, i, c)
             new_k = -(-width(i) // P)
             for t in range(ready_k, new_k):
                 if (load_k, t) not in early:
@@ -446,6 +461,7 @@ def tile_chunkedattention_pa_kernel(tc, q, k_means, v_means, intra, wo, bo, out)
             due(40 + 2 * h, group_v, h)
         due(40 + 24, quantise_v)
 
+        turns = [steps.index(step) for step in (turn_wo, turn_f, turn_e, turn_q, turn_k)]
         for tick in sorted(plan):
-            for number, what in sorted(plan[tick], key=lambda item: item[0]):
+            for number, what in sorted(plan[tick], key=lambda item: (tick % 2 == 1 or item[0] not in turns, item[0])):
                 steps[number](*what)

@@ -244,16 +244,17 @@ def tile_chunkedattention_pa_kernel(tc, q, k_means, v_means, intra, wo, bo, out)
             top_s[i, h0] = small.tile([P, n], F32, name="top_s")
             shift[i, h0] = small.tile([P, n], F32, name="shift")
             if n == 1:
-                minus_s[i, h0] = work.tile([P, CHUNKS], F32, name="minus_s")
-                nc.vector.tensor_scalar(
-                    out=minus_s[i, h0][:, 0:w],
-                    in0=s_ps[i, h0][:, 0, 0:w],
-                    scalar1=-SCALE,
-                    scalar2=None,
-                    op0=ALU.mult,
-                    op1=ALU.min,
-                    accum_out=shift[i, h0][:],
-                )
+                minus_s[i, h0] = work.tile([P, n, CHUNKS // n], F32, name="minus_s")
+                for b in range(n):
+                    nc.vector.tensor_scalar(
+                        out=minus_s[i, h0][:, b, 0:w],
+                        in0=s_ps[i, h0][:, b, 0:w],
+                        scalar1=-SCALE,
+                        scalar2=None,
+                        op0=ALU.mult,
+                        op1=ALU.min,
+                        accum_out=shift[i, h0][:, b : b + 1],
+                    )
                 return
             nc.vector.tensor_reduce(out=top_s[i, h0][:], in_=s_ps[i, h0][:, :, 0:w], axis=AXIS.X, op=ALU.max)
             nc.gpsimd.tensor_scalar(out=shift[i, h0][:], in0=top_s[i, h0][:], scalar1=-SCALE, scalar2=None, op0=ALU.mult)
@@ -263,7 +264,7 @@ def tile_chunkedattention_pa_kernel(tc, q, k_means, v_means, intra, wo, bo, out)
             for b in range(n):
                 nc.scalar.activation(
                     out=e_tile(i, h0)[:, b, 0:w],
-                    in_=minus_s[i, h0][:, 0:w] if n == 1 else s_ps[i, h0][:, b, 0:w],
+                    in_=(minus_s if n == 1 else s_ps)[i, h0][:, b, 0:w],
                     func=ACT.Exp,
                     bias=shift[i, h0][:, b : b + 1],
                     scale=-1.0 if n == 1 else SCALE,
@@ -390,7 +391,7 @@ def tile_chunkedattention_pa_kernel(tc, q, k_means, v_means, intra, wo, bo, out)
 
         steps = [load_k, load_q, load_v_shared, load_intra, load_wo, load_bias, load_v, top, finish, quantise_f, fuse, invert, quantise_e, quantise_v_shared, spread_v, quantise_v, quantise_wo, group_f, group_e, exponent, keep_q, keep_k, group_wo, finish_aside, group_v, group_v_shared, score, project, attend, turn_wo, turn_f, turn_e, turn_q, turn_k]
         plan = {}
-        early = [(load_k, 0), (load_q, 0), (load_v_shared, 4, 0), (load_v_shared, 4, 1), (load_v_shared, 4, 2), (load_v_shared, 4, 3), (load_q, 1), (load_intra, 0), (load_wo, 0), (load_q, 2), (load_wo, 2), (load_intra, 1), (load_wo, 4), (load_q, 3), (load_wo, 6), (load_intra, 2), (load_k, 1), (load_q, 4), (load_v_shared, 2, 0), (load_v_shared, 2, 1), (load_bias,), (load_intra, 3), (load_q, 5)]
+        early = [(load_k, 0), (load_q, 0), (load_q, 1), (load_v_shared, 4, 0), (load_v_shared, 4, 1), (load_v_shared, 4, 2), (load_v_shared, 4, 3), (load_wo, 0), (load_intra, 0), (load_q, 2), (load_wo, 2), (load_wo, 4), (load_intra, 1), (load_q, 3), (load_wo, 6), (load_k, 1), (load_q, 4), (load_intra, 2), (load_v_shared, 2, 0), (load_v_shared, 2, 1), (load_bias,), (load_intra, 3), (load_q, 5)]
         for load in early:
             load[0](*load[1:])
 
@@ -413,7 +414,7 @@ def tile_chunkedattention_pa_kernel(tc, q, k_means, v_means, intra, wo, bo, out)
                 due(at + 1, top, i, h0)
                 due(at + (3 if n == 1 else 2), exponent, i, h0)
             for h0 in range(0, HEADS, 2 * n):
-                turned = first + h0 * ticks // HEADS + {4: 10, 2: 8, 1: 8}[n]
+                turned = first + h0 * ticks // HEADS + {4: 10, 2: 8, 1: 7}[n]
                 due(turned, turn_e, i, h0)
                 due(turned + 2, group_e, i, h0)
                 due(turned + 4, quantise_e, i, h0)
@@ -456,10 +457,10 @@ def tile_chunkedattention_pa_kernel(tc, q, k_means, v_means, intra, wo, bo, out)
             due(tick + (4 if n == 4 else 14) + 2, spread_v, n)
         for u in range(2):
             if (load_v, u) not in early:
-                due(40 - 40, load_v, u)
+                due(38 - 38, load_v, u)
         for h in range(HEADS):
-            due(40 + 2 * h, group_v, h)
-        due(40 + 24, quantise_v)
+            due(38 + 3 * h, group_v, h)
+        due(38 + 30, quantise_v)
 
         turns = [steps.index(step) for step in (turn_wo, turn_f, turn_e, turn_q, turn_k)]
         for tick in sorted(plan):

import math
from contextlib import ExitStack

import concourse.mybir as mybir
from concourse.masks import make_identity

BF16 = mybir.dt.bfloat16
F32 = mybir.dt.float32
I32 = mybir.dt.int32
U32 = mybir.dt.uint32
U8 = mybir.dt.uint8
FP8X4 = mybir.dt.float8_e4m3fn_x4
ACT = mybir.ActivationFunctionType
ALU = mybir.AluOpType
AXIS = mybir.AxisListType

P = 128
PACK = 4
HEADS = 8
D = 128
CHUNKS = 512
PLACES = 4
TOKENS = CHUNKS * PLACES
E = HEADS * D
TILES = TOKENS // P
TILE_CHUNKS = P // PLACES
GROUPS = E // (P * PACK)
HALF = 512
SCALE = 1.0 / math.sqrt(D)
MASKED = -1.0e30

FLOPS = 2 * HEADS * TOKENS * CHUNKS * D * 2 + 2 * TOKENS * E * E


def width(i):
    return TILE_CHUNKS * (i + 1)


def share(i):
    return 4 if width(i) <= 128 else 2 if width(i) <= 256 else 1


ORDER = list(range(TILES))


def tile_chunkedattention_pa_kernel(tc, q, k_means, v_means, intra, wo, bo, out):
    nc = tc.nc
    q_rows = q.rearrange("b h c t d -> (b h) (c t) d")
    intra_rows = intra.rearrange("b h c t d -> (b h) (c t) d")
    k_blocks = k_means.rearrange("b h (t p) d -> t p (b h) d", p=P)
    v_blocks = v_means.rearrange("b h (u p e) d -> u p (b h) e d", p=P, e=2)
    out_rows = out.rearrange("b s o -> (b s) o")

    with ExitStack() as ctx:
        ctx.enter_context(tc.manual_schedule())
        keep = ctx.enter_context(tc.tile_pool(name="keep", bufs=1))
        work = ctx.enter_context(tc.tile_pool(name="work", bufs=4))
        small = ctx.enter_context(tc.tile_pool(name="small", bufs=6))
        rows_in = ctx.enter_context(tc.tile_pool(name="rows_in", bufs=6))
        store = ctx.enter_context(tc.tile_pool(name="store", bufs=4))
        turn_ps = ctx.enter_context(tc.psum_pool(name="turn_ps", bufs=3))
        score_ps = ctx.enter_context(tc.psum_pool(name="score_ps", bufs=3))
        mx_ps = ctx.enter_context(tc.psum_pool(name="mx_ps", bufs=2))

        k_sb = keep.tile([P, PACK, HEADS, D], BF16)
        wo_sb = keep.tile([P, E // P, E], BF16)
        bias = keep.tile([P, E], BF16)
        q_sb, intra_sb = {}, {}
        v_sb = {
            1: keep.tile([P, 2, HEADS, 2, D], BF16, name="v_sb1"),
            2: keep.tile([P, HEADS // 2, PACK, D], BF16, name="v_sb2"),
            4: keep.tile([P, HEADS // 4, PACK, D], BF16, name="v_sb4"),
        }

        wo_blocks = wo.rearrange("(a p) k -> a p k", p=P)

        def load_q(i):
            q_sb[i] = rows_in.tile([P, HEADS, D], BF16, name="q_sb")
            nc.sync.dma_start(out=q_sb[i][:], in_=q_rows[:, i * P : (i + 1) * P, :].rearrange("h p d -> p h d"))

        def load_intra(i):
            intra_sb[i] = rows_in.tile([P, HEADS, D], BF16, name="intra_sb")
            nc.sync.dma_start(out=intra_sb[i][:], in_=intra_rows[:, i * P : (i + 1) * P, :].rearrange("h p d -> p h d"))

        def load_k(t):
            nc.sync.dma_start(out=k_sb[:, t], in_=k_blocks[t])

        def load_wo(a):
            nc.sync.dma_start(out=wo_sb[:, a : a + 2, :], in_=wo_blocks[a : a + 2].rearrange("a p k -> p a k"))

        def load_bias():
            nc.sync.dma_start(out=bias[:], in_=bo.partition_broadcast(P))

        def load_v(u):
            nc.sync.dma_start(out=v_sb[1][:, u], in_=v_blocks[u])

        def load_v_shared(n, s):
            rows = P // n
            heads = v_means.rearrange("b (a s) j d -> s (b a) j d", s=n)
            nc.sync.dma_start(
                out=v_sb[n][s * rows : (s + 1) * rows],
                in_=heads[s, :, 0 : rows * PACK, :].rearrange("a (p t) d -> p a t d", t=PACK),
            )

        warm = small.tile([P, 1], F32)
        nc.vector.memset(warm[:], 0.0)
        nc.scalar.activation(out=warm[:], in_=warm[:], func=ACT.Exp)

        ident = keep.tile([P, P], BF16)
        make_identity(nc, ident[:])
        ident_f32 = keep.tile([P, P], F32)
        make_identity(nc, ident_f32[:])
        mask_f32 = keep.tile([P, TILE_CHUNKS], F32)
        nc.gpsimd.memset(mask_f32[:], 0.0)
        nc.gpsimd.affine_select(
            out=mask_f32[:],
            in_=mask_f32[:],
            pattern=[[-PLACES, TILE_CHUNKS]],
            compare_op=ALU.is_ge,
            fill=MASKED,
            base=0,
            channel_multiplier=1,
        )
        mask = keep.tile([P, TILE_CHUNKS], BF16)

        e_sets = {4: 8, 2: 4, 1: 8}
        e_sb, v_codes = {}, {}
        for n in (4, 2, 1):
            e_sb[n] = [keep.tile([P, n, CHUNKS // n], BF16, name="e_sb%d_%d" % (n, r)) for r in range(e_sets[n])]
            v_codes[n] = keep.tile([P, HEADS, D], U32, align_bytes=64, name="v_codes%d" % n)

        for n, lowest, per_tile in ((4, 0, 2), (2, 4, 0), (1, 8, 0)):
            for r in range(e_sets[n]):
                never = e_sb[n][r][:].bitcast(F32)[:, :, width(lowest + (r // 2 if per_tile else 0)) // 2 :]
                if never.shape[2]:
                    nc.vector.memset(never, 0.0)
            if n > 1:
                nc.vector.memset(v_codes[n][:], 0)

        nc.vector.tensor_copy(out=mask[:], in_=mask_f32[:])

        k_t = keep.tile([P, HEADS, CHUNKS], BF16)

        k_ps = {}

        def turn_k(t):
            k_ps[t] = turn_ps.tile([P, HEADS, P], BF16, tag="turn", name="k_ps")
            for h in range(HEADS):
                nc.tensor.transpose(k_ps[t][:, h, :], k_sb[:, t, h, :], ident[:])

        def keep_k(t):
            nc.scalar.copy(out=k_t[:, :, t * P : (t + 1) * P], in_=k_ps[t][:])

        def copy_gpsimd(out, in_):
            nc.gpsimd.tensor_scalar(out=out, in0=in_, scalar1=1.0, scalar2=0.0, op0=ALU.mult, op1=ALU.add)

        v_grouped = {1: keep.tile([P, HEADS, D, PACK], BF16, align_bytes=64, name="v_grouped1")}
        v_scales = {1: keep.tile([P, HEADS, D], U8, align_bytes=64, name="v_scales1")}
        v_dense = {}
        for n in (2, 4):
            v_grouped[n] = keep.tile([P, HEADS // n, D, PACK], BF16, align_bytes=64, name="v_grouped%d" % n)
            v_scales[n] = keep.tile([P, HEADS // n, D], U8, align_bytes=64, name="v_scales%d" % n)
            v_dense[n] = keep.tile([P, HEADS // n, D], U32, align_bytes=64, name="v_dense%d" % n)

        def group_v_shared(n, a):
            (nc.vector.tensor_copy if n == 4 else nc.scalar.copy)(out=v_grouped[n][:, a], in_=v_sb[n][:, a].rearrange("p t d -> p d t"))

        def quantise_v_shared(n):
            nc.vector.quantize_mx(
                out=v_dense[n][:].rearrange("p a d -> p (a d)").bitcast(FP8X4),
                scales=v_scales[n][:].rearrange("p a d -> p (a d)"),
                in_=v_grouped[n][:].rearrange("p a d t -> p (a d t)"),
            )

        def spread_v(n):
            rows = P // n
            heads = v_codes[n][:].rearrange("p (a s) d -> p a s d", s=n)
            for s in range(n):
                part = slice(s * rows, (s + 1) * rows)
                nc.vector.tensor_copy(out=heads[part, :, s, :].bitcast(I32), in_=v_dense[n][part].bitcast(I32))

        def group_v(h):
            nc.scalar.copy(out=v_grouped[1][:, h].rearrange("p d (u e) -> p d u e", e=2), in_=v_sb[1][:, :, h].rearrange("p u e d -> p d u e"))

        def quantise_v():
            nc.vector.quantize_mx(
                out=v_codes[1][:].rearrange("p h d -> p (h d)").bitcast(FP8X4),
                scales=v_scales[1][:].rearrange("p h d -> p (h d)"),
                in_=v_grouped[1][:].rearrange("p h d t -> p (h d t)"),
            )

        wo_grouped = keep.tile([P, GROUPS, E, PACK], BF16, align_bytes=64)
        wo_codes = keep.tile([P, GROUPS, E], U32, align_bytes=64)
        wo_scales = keep.tile([P, GROUPS, E], U8, align_bytes=64)

        wo_ps = {}

        def turn_wo(a):
            wo_ps[a] = mx_ps.tile([P, GROUPS * 2, P], F32, tag="mx", name="wo_ps")
            for b in range(GROUPS * 2):
                nc.tensor.transpose(wo_ps[a][:, b, :], wo_sb[:, a, :].bitcast(F32)[:, b * P : (b + 1) * P], ident_f32[:])

        def group_wo(a):
            (nc.vector.tensor_copy if a % 2 == 0 else nc.scalar.copy)(
                out=wo_grouped[:, :, a * P : (a + 1) * P, :].bitcast(F32),
                in_=wo_ps[a][:].rearrange("p (g u) o -> p g o u", u=2),
            )

        def quantise_wo(g):
            nc.vector.quantize_mx(
                out=wo_codes[:, g, :].bitcast(FP8X4),
                scales=wo_scales[:, g, :],
                in_=wo_grouped[:, g].rearrange("p o t -> p (o t)"),
            )

        minus_s, q_ps, q_t, s_ps, top_s, shift, sums = {}, {}, {}, {}, {}, {}, {}
        e_ps, e_grouped, e_codes, e_scales, i_ps, over_sum, fused = {}, {}, {}, {}, {}, {}, {}
        f_ps, f_grouped, f_codes, f_scales, o_ps = {}, {}, {}, {}, {}

        def turn_q(i):
            q_ps[i] = turn_ps.tile([P, HEADS, P], BF16, tag="turn", name="q_ps")
            for h in range(HEADS):
                nc.tensor.transpose(q_ps[i][:, h, :], q_sb[i][:, h, :], ident[:])

        def keep_q(i):
            q_t[i] = work.tile([P, HEADS, P], BF16, name="q_t")
            nc.scalar.copy(out=q_t[i][:], in_=q_ps[i][:])
            sums[i] = small.tile([P, HEADS], F32, name="sums")

        def e_tile(i, h):
            n = share(i)
            return e_sb[n][(i * (HEADS // n) + h // n) % e_sets[n]]

        def score(i, h0):
            n, w = share(i), width(i)
            s_ps[i, h0] = score_ps.tile([P, n, CHUNKS // n], F32, name="s_ps")
            for b in range(n):
                bank = s_ps[i, h0][:, b, :]
                nc.tensor.matmul(bank[:, 0:w], lhsT=q_t[i][:, h0 + b, :], rhs=k_t[:, h0 + b, 0:w], start=True, stop=False)
                nc.tensor.matmul(bank[:, w - TILE_CHUNKS : w], lhsT=ident[:], rhs=mask[:], start=False, stop=True)

        def top(i, h0):
            n, w = share(i), width(i)
            top_s[i, h0] = small.tile([P, n], F32, name="top_s")
            shift[i, h0] = small.tile([P, n], F32, name="shift")
            if n == 1:
                minus_s[i, h0] = work.tile([P, n, CHUNKS // n], F32, name="minus_s")
                for b in range(n):
                    nc.vector.tensor_scalar(
                        out=minus_s[i, h0][:, b, 0:w],
                        in0=s_ps[i, h0][:, b, 0:w],
                        scalar1=-SCALE,
                        scalar2=None,
                        op0=ALU.mult,
                        op1=ALU.min,
                        accum_out=shift[i, h0][:, b : b + 1],
                    )
                return
            nc.vector.tensor_reduce(out=top_s[i, h0][:], in_=s_ps[i, h0][:, :, 0:w], axis=AXIS.X, op=ALU.max)
            nc.gpsimd.tensor_scalar(out=shift[i, h0][:], in0=top_s[i, h0][:], scalar1=-SCALE, scalar2=None, op0=ALU.mult)

        def exponent(i, h0):
            n, w = share(i), width(i)
            for b in range(n):
                nc.scalar.activation(
                    out=e_tile(i, h0)[:, b, 0:w],
                    in_=(minus_s if n == 1 else s_ps)[i, h0][:, b, 0:w],
                    func=ACT.Exp,
                    bias=shift[i, h0][:, b : b + 1],
                    scale=-1.0 if n == 1 else SCALE,
                    accum_out=sums[i][:, h0 + b : h0 + b + 1],
                )

        def run_of(i, h):
            units = 4 if share(i) == 1 else 2
            heads = units * share(i)
            return h // heads * heads, units

        def turn_e(i, h0):
            n = share(i)
            e_ps[i, h0] = turn_ps.tile([P, 2, 2, P], F32, tag="turn", name="e_ps")
            for b in range(2):
                words = e_tile(i, h0 + b * n)[:].rearrange("p n j -> p (n j)").bitcast(F32)
                for u in range(2):
                    part = words[:, u * P : (u + 1) * P] if n == 1 else words[:, u : 2 * P : 2]
                    nc.tensor.transpose(e_ps[i, h0][:, b, u, :], part, ident_f32[:])

        def group_e(i, h0):
            first, units = run_of(i, h0)
            if h0 == first:
                e_grouped[i, h0] = work.tile([P, units, P, PACK], BF16, align_bytes=64, name="e_grouped%d" % units, bufs=3)
            place = (h0 - first) // share(i)
            nc.scalar.copy(
                out=e_grouped[i, first][:, place : place + 2].bitcast(F32), in_=e_ps[i, h0][:].rearrange("p b u r -> p b r u")
            )

        def quantise_e(i, h0):
            first, units = run_of(i, h0)
            if h0 + 2 * share(i) < first + units * share(i):
                return
            h0 = first
            e_codes[i, h0] = work.tile([P, units, P], U32, align_bytes=64, name="e_codes%d" % units)
            e_scales[i, h0] = work.tile([P, units, P], U8, align_bytes=64, name="e_scales%d" % units)
            nc.vector.quantize_mx(
                out=e_codes[i, h0][:].rearrange("p b r -> p (b r)").bitcast(FP8X4),
                scales=e_scales[i, h0][:].rearrange("p b r -> p (b r)"),
                in_=e_grouped[i, h0][:].rearrange("p b r t -> p (b r t)"),
            )

        def attend(i, h0):
            n = share(i)
            i_ps[i, h0] = mx_ps.tile([P, PACK, D], F32, tag="mx", name="i_ps")
            for t in range(PACK):
                h = h0 + t
                first, units = run_of(i, h)
                pair = (i, first)
                b = (h - first) // n
                nc.tensor.matmul_mx(
                    out=i_ps[i, h0][:, t, :],
                    lhsT=e_codes[pair][:, b, :].bitcast(FP8X4),
                    lhsT_scale=e_scales[pair][:, b, :],
                    rhs=v_codes[n][:, h, :].bitcast(FP8X4),
                    rhs_scale=v_scales[n][:, h // n, :],
                    start=True,
                    stop=True,
                )

        def invert(i):
            over_sum[i] = small.tile([P, HEADS], F32, name="over_sum")
            nc.vector.reciprocal(out=over_sum[i][:], in_=sums[i][:])

        def fuse(i, h0, heads):
            if h0 + heads[0] == 0:
                fused[i] = work.tile([P, HEADS, D], BF16, name="fused")
            for t in heads:
                h = h0 + t
                nc.vector.scalar_tensor_tensor(
                    out=fused[i][:, h, :],
                    in0=i_ps[i, h0][:, t, :],
                    scalar=over_sum[i][:, h : h + 1],
                    in1=intra_sb[i][:, h, :],
                    op0=ALU.mult,
                    op1=ALU.add,
                )

        def turn_f(i):
            f_ps[i] = turn_ps.tile([P, GROUPS * 2, P], F32, tag="turn", name="f_ps")
            words = fused[i][:].rearrange("p h d -> p (h d)").bitcast(F32)
            for b in range(GROUPS * 2):
                nc.tensor.transpose(f_ps[i][:, b, :], words[:, b * P : (b + 1) * P], ident_f32[:])

        def group_f(i):
            f_grouped[i] = work.tile([P, GROUPS, P, PACK], BF16, align_bytes=64, name="f_grouped")
            nc.scalar.copy(out=f_grouped[i][:].bitcast(F32), in_=f_ps[i][:].rearrange("p (g u) r -> p g r u", u=2))

        def quantise_f(i):
            f_codes[i] = work.tile([P, GROUPS, P], U32, align_bytes=64, name="f_codes")
            f_scales[i] = work.tile([P, GROUPS, P], U8, align_bytes=64, name="f_scales")
            nc.vector.quantize_mx(
                out=f_codes[i][:].rearrange("p g r -> p (g r)").bitcast(FP8X4),
                scales=f_scales[i][:].rearrange("p g r -> p (g r)"),
                in_=f_grouped[i][:].rearrange("p g r t -> p (g r t)"),
            )

        def project(i, c):
            o_ps[i, c] = mx_ps.tile([P, HALF], F32, tag="mx", name="o_ps")
            for g in range(GROUPS):
                nc.tensor.matmul_mx(
                    out=o_ps[i, c][:],
                    lhsT=f_codes[i][:, g, :].bitcast(FP8X4),
                    lhsT_scale=f_scales[i][:, g, :],
                    rhs=wo_codes[:, g, c * HALF : (c + 1) * HALF].bitcast(FP8X4),
                    rhs_scale=wo_scales[:, g, c * HALF : (c + 1) * HALF],
                    start=(g == 0),
                    stop=(g == GROUPS - 1),
                )

        def finish(i, c):
            cols = slice(c * HALF, (c + 1) * HALF)
            result = store.tile([P, HALF], F32, name="result")
            nc.vector.tensor_tensor(out=result[:], in0=o_ps[i, c][:], in1=bias[:, cols], op=ALU.add)
            nc.sync.dma_start(out=out_rows[i * P : (i + 1) * P, cols], in_=result[:])

        def finish_aside(i, c):
            cols = slice(c * HALF, (c + 1) * HALF)
            product = store.tile([P, HALF], F32, name="product", bufs=2)
            nc.scalar.copy(out=product[:], in_=o_ps[i, c][:])
            result = store.tile([P, HALF], F32, name="result")
            nc.gpsimd.tensor_tensor(out=result[:], in0=product[:], in1=bias[:, cols], op=ALU.add)
            nc.sync.dma_start(out=out_rows[i * P : (i + 1) * P, cols], in_=result[:])

        steps = [load_k, load_q, load_v_shared, load_intra, load_wo, load_bias, load_v, top, finish, quantise_f, fuse, invert, quantise_e, quantise_v_shared, spread_v, quantise_v, quantise_wo, group_f, group_e, exponent, keep_q, keep_k, group_wo, finish_aside, group_v, group_v_shared, score, project, attend, turn_wo, turn_f, turn_e, turn_q, turn_k]
        plan = {}
        early = [(load_k, 0), (load_q, 0), (load_q, 1), (load_v_shared, 4, 0), (load_v_shared, 4, 1), (load_v_shared, 4, 2), (load_v_shared, 4, 3), (load_wo, 0), (load_intra, 0), (load_q, 2), (load_wo, 2), (load_wo, 4), (load_intra, 1), (load_q, 3), (load_wo, 6), (load_k, 1), (load_q, 4), (load_intra, 2), (load_v_shared, 2, 0), (load_v_shared, 2, 1), (load_bias,), (load_intra, 3), (load_q, 5)]
        for load in early:
            load[0](*load[1:])

        def due(tick, step, *what):
            plan.setdefault(tick, []).append((steps.index(step), what))

        first = 0
        ready_k = 0
        for place, i in enumerate(ORDER):
            n = share(i)
            ticks = {4: 8, 2: 8, 1: 8}[n]
            for step, lead in ((load_q, 30), (load_intra, 20)):
                if (step, i) not in early:
                    due(first - lead, step, i)
            due(first - 5, turn_q, i)
            due(first - 3, keep_q, i)
            for h0 in range(0, HEADS, n):
                at = first + h0 * ticks // HEADS
                due(at, score, i, h0)
                due(at + 1, top, i, h0)
                due(at + (3 if n == 1 else 2), exponent, i, h0)
            for h0 in range(0, HEADS, 2 * n):
                turned = first + h0 * ticks // HEADS + {4: 10, 2: 8, 1: 7}[n]
                due(turned, turn_e, i, h0)
                due(turned + 2, group_e, i, h0)
                due(turned + 4, quantise_e, i, h0)
            due(first + 14, invert, i)
            for x in range(HEADS // PACK):
                at = first + 16 + x * ticks // 2
                due(at, attend, i, x * PACK)
                due(at + 2, fuse, i, x * PACK, (0, 1))
                due(at + 2, fuse, i, x * PACK, (2, 3))
            done = first + 16 + ticks // 2 + 2 + 0
            due(done + 3, turn_f, i)
            due(done + 3 + 2, group_f, i)
            due(done + 3 + 4, quantise_f, i)
            for c in range(E // HALF):
                due(done + 12 + c * ticks // 2, project, i, c)
                if c == 1 and 3 < i < 12:
                    due(done + 12 + c * ticks // 2 + 1, finish_aside, i, c)
                else:
                    due(done + 12 + c * ticks // 2 + 2, finish, i, c)
            new_k = -(-width(i) // P)
            for t in range(ready_k, new_k):
                if (load_k, t) not in early:
                    due(first - 34, load_k, t)
                due(first - 9 - 2 * (new_k - 1 - t), turn_k, t)
                due(first - 9 - 2 * (new_k - 1 - t) + 2, keep_k, t)
            ready_k = max(ready_k, new_k)
            first += ticks
        for a in range(E // P):
            due(2 * a + 9, turn_wo, a)
            due(2 * a + 9 + 2, group_wo, a)
        for g in range(GROUPS):
            due(28 + 2 * g, quantise_wo, g)
        for n, tick in ((4, 4), (2, 28)):
            for s in range(n):
                if (load_v_shared, n, s) not in early:
                    due(tick - 12, load_v_shared, n, s)
            for a in range(HEADS // n):
                due(tick + 2 * a, group_v_shared, n, a)
            due(tick + (4 if n == 4 else 14), quantise_v_shared, n)
            due(tick + (4 if n == 4 else 14) + 2, spread_v, n)
        for u in range(2):
            if (load_v, u) not in early:
                due(38 - 38, load_v, u)
        for h in range(HEADS):
            due(38 + 3 * h, group_v, h)
        due(38 + 30, quantise_v)

        turns = [steps.index(step) for step in (turn_wo, turn_f, turn_e, turn_q, turn_k)]
        for tick in sorted(plan):
            for number, what in sorted(plan[tick], key=lambda item: (tick % 2 == 1 or item[0] not in turns, item[0])):
                steps[number](*what)
